import numpy as np
import ml_dtypes


def mxq(x, axis, fmt="e4m3"):
    dtype, down = {"e4m3": (ml_dtypes.float8_e4m3fn, 7), "e5m2": (ml_dtypes.float8_e5m2, 14)}[fmt]
    v = np.moveaxis(np.asarray(x, np.float32).astype(ml_dtypes.bfloat16).astype(np.float64), axis, -1)
    blocks = v.reshape(v.shape[:-1] + (-1, 32))
    amax = np.abs(blocks).max(-1, keepdims=True)
    byte = np.maximum(np.where(amax > 0, np.frexp(amax)[1] - 1 + 127, 0) - down, 1)
    scale = np.exp2(byte - 127.0)
    codes = (blocks / scale).astype(np.float32).astype(dtype).astype(np.float64)
    return np.moveaxis((codes * scale).reshape(v.shape), -1, axis)


WIDE = False


def mx_kscale(k):
    if not WIDE:
        return np.ones(k)
    levels = np.array([10, -10, 5, -5, 0])
    if k % 512:
        return np.exp2(np.random.permutation(np.resize(levels, k // 32))).repeat(32)
    a = np.empty((k // 512, 16))
    for p in range(k // 512):
        a[p, :8] = np.random.permutation(np.resize(levels, 8))
        for g in range(8):
            far = levels[np.abs(levels - a[p, g]) >= 10]
            a[p, g + 8] = far[np.random.randint(len(far))]
    return np.exp2(a.ravel()).repeat(32)


BF16 = ml_dtypes.bfloat16


def bf(x):
    return np.asarray(x, np.float32).astype(BF16)


def f64(x):
    return np.asarray(x).astype(np.float64)


B, T, C, H, NOPE, ROPE, VD, LORA = 1, 512, 2048, 16, 128, 128, 128, 512
EPS = 1e-6
HALF = ROPE // 2
KVW = H * (NOPE + VD)


def make_freq_cis():
    inv = 1.0 / (10000.0 ** (np.arange(0, ROPE, 2) / ROPE))
    ang = np.outer(np.arange(T), inv)
    return np.stack([np.cos(ang), np.sin(ang)], -1)


def apply_rope(v, fc):
    vr = v.reshape(B, T, HALF, 2)
    real = vr[..., 0] * fc[..., 0] - vr[..., 1] * fc[..., 1]
    imag = vr[..., 1] * fc[..., 0] + vr[..., 0] * fc[..., 1]
    return np.stack([real, imag], -1).reshape(B, T, ROPE)


def draw0():
    s, t = mx_kscale(C), mx_kscale(LORA)
    return {"x": bf(np.random.standard_normal((B, T, C)) * s),
            "freq_cis": bf(make_freq_cis()),
            "Wckv": bf(np.random.standard_normal((C, LORA + ROPE)) / np.sqrt(C) / s[:, None]),
            "kv_norm_w": bf((1.0 + 0.1 * np.random.standard_normal(LORA)) * t),
            "Wdkv": bf(np.random.standard_normal((LORA, KVW)) / np.sqrt(LORA) / t[:, None])}


def core(x, freq_cis, Wckv, kv_norm_w, Wdkv):
    ckv = mxq(f64(x), 2, "e4m3") @ mxq(f64(Wckv), 0, "e4m3")
    kv_lat, k_rope = ckv[..., :LORA], ckv[..., LORA:]
    k_rope = apply_rope(k_rope, f64(freq_cis))
    lat_n = kv_lat / np.sqrt(np.mean(kv_lat * kv_lat, -1, keepdims=True) + EPS) * f64(kv_norm_w)
    kv = mxq(lat_n, 2, "e4m3") @ mxq(f64(Wdkv), 0, "e4m3")
    return kv, k_rope


def e4m3fn_bytes(y):
    return np.clip(np.asarray(y, np.float64), -448.0, 448.0).astype(np.float32).astype(ml_dtypes.float8_e4m3fn).view(np.uint8)


def e4m3fn_values(b):
    return np.asarray(b, np.uint8).view(ml_dtypes.float8_e4m3fn).astype(np.float64)


def setup_inputs():
    d = draw0()
    x0 = np.asarray(d['Wdkv']).astype(np.float64)
    s = (np.max(np.abs(x0), axis=(1,), keepdims=True) / 448.0).astype(np.float32)
    out = {}
    for k, v in d.items():
        if k == 'Wdkv':
            out['Wdkv_bytes'] = e4m3fn_bytes(x0 / s.astype(np.float64))
            out['Wdkv_scale'] = s
        else:
            out[k] = v
    return out


def reference(x, freq_cis, Wckv, kv_norm_w, Wdkv_bytes, Wdkv_scale):
    return core(x, freq_cis, Wckv, kv_norm_w, e4m3fn_values(Wdkv_bytes) * Wdkv_scale.astype(np.float64))

@@ -1,0 +1,298 @@
+from contextlib import ExitStack
+
+import concourse.mybir as mybir
+from concourse.masks import make_identity
+
+T, C, LORA, ROPE, KVW = 512, 2048, 512, 128, 4096
+WIDTH = LORA + ROPE
+FLOPS = 2 * T * C * WIDTH + 2 * T * LORA * KVW
+
+F32 = mybir.dt.float32
+BF16 = mybir.dt.bfloat16
+U32 = mybir.dt.uint32
+U8 = mybir.dt.uint8
+FP8 = mybir.dt.float8_e4m3fn
+FP8X4 = mybir.dt.float8_e4m3fn_x4
+ALU = mybir.AluOpType
+ACT = mybir.ActivationFunctionType
+
+P = 128
+NB = T // P
+NP = C // 512
+APL = [1, 1, 1, 1, 1, 1, 1, 1, 1]
+CHUNKS = [(512 * c, 512) for c in range(7)] + [(3584, 256), (3840, 256)]
+NCH = len(CHUNKS)
+BLOADS = [(0, 512), (512, 512), (1024, 1024), (2048, 2048)]
+SPLIT = 448
+
+
+def tile_multiheadlatentattention_pa_kernel(tc, x, freq_cis, Wckv, kv_norm_w, Wdkv_bytes, Wdkv_scale, out_0, out_1):
+    nc = tc.nc
+    xf = x.flatten_outer_dims()
+    kvf = out_0.flatten_outer_dims()
+    krf = out_1.flatten_outer_dims()
+
+    with ExitStack() as ctx:
+        keep = ctx.enter_context(tc.tile_pool(name="keep", bufs=1))
+        work = ctx.enter_context(tc.tile_pool(name="work", bufs=3))
+        outs = ctx.enter_context(tc.tile_pool(name="outs", bufs=12))
+        psum = ctx.enter_context(tc.psum_pool(name="psum", bufs=1))
+        ctx.enter_context(tc.manual_schedule())
+
+        ident = keep.tile([P, P], F32, name="ident")
+        ones = keep.tile([P, P], BF16, name="ones")
+        grow = keep.tile([P, LORA], BF16, name="grow")
+        gain = keep.tile([P, LORA], F32, name="gain")
+        eps = keep.tile([P, 1], F32, name="eps")
+        dummy = keep.tile([P, 1], F32, name="dummy")
+        scale = keep.tile([P, 4], F32, name="scale")
+        fr = keep.tile([P, NB * 64, 2], BF16, name="fr")
+        ss = keep.tile([P, NB * 64, 2], F32, name="ss")
+        xraw = [keep.tile([P, C], BF16, name="xraw%d" % b) for b in range(NB)]
+        wraw = [keep.tile([P, 4, WIDTH], BF16, name="wraw%d" % g) for g in range(NP)]
+        wb = [keep.tile([P, 4, n], U8, name="wb%d" % i) for i, (o, n) in enumerate(BLOADS)]
+        xc = [keep.tile([P, NP, P], U32, name="xc%d" % b, align_bytes=64) for b in range(NB)]
+        xs = [keep.tile([P, NP, P], U8, name="xs%d" % b, align_bytes=64) for b in range(NB)]
+        wc = [keep.tile([P, WIDTH], U32, name="wc%d" % g, align_bytes=64) for g in range(NP)]
+        ws = [keep.tile([P, WIDTH], U8, name="ws%d" % g, align_bytes=64) for g in range(NP)]
+        ncod = [keep.tile([P, P], U32, name="ncod%d" % b, align_bytes=64) for b in range(NB)]
+        nsc = [keep.tile([P, P], U8, name="nsc%d" % b, align_bytes=64) for b in range(NB)]
+        dc = [keep.tile([P, CHUNKS[c][1]], U32, name="dc%d" % c, align_bytes=64) for c in range(NCH)]
+        ds = [keep.tile([P, CHUNKS[c][1]], U8, name="ds%d" % c, align_bytes=64) for c in range(NCH)]
+        sumsq = [keep.tile([P, 1], F32, name="sumsq%d" % b) for b in range(NB)]
+        rstd = [keep.tile([P, 1], F32, name="rstd%d" % b) for b in range(NB)]
+
+        wv = Wckv.rearrange("(g p j) n -> g p j n", p=P, j=4)
+        bv = Wdkv_bytes.rearrange("(p j) n -> p j n", j=4)
+
+        def load_x(b):
+            nc.sync.dma_start(out=xraw[b][:], in_=xf[b * P : (b + 1) * P, :])
+
+        def load_w(g):
+            nc.sync.dma_start(out=wraw[g][:], in_=wv[g])
+
+        nc.vector.memset(grow[:], 0.0)
+        nc.scalar.dma_start(out=grow[0:1, :], in_=kv_norm_w.rearrange("(o n) -> o n", o=1))
+        nc.scalar.dma_start(out=scale[:], in_=Wdkv_scale.rearrange("(p j) o -> p (j o)", j=4))
+        def load_b(c):
+            o, n = BLOADS[c]
+            nc.sync.dma_start(out=wb[c][:], in_=bv[:, :, o : o + n])
+
+        for g in range(NP):
+            load_w(g)
+        load_x(0)
+        load_x(1)
+        load_b(0)
+        load_x(2)
+        load_b(1)
+        load_x(3)
+        load_b(2)
+        load_b(3)
+        nc.sync.dma_start(
+            out=fr[:].rearrange("p (b i) e -> p b (i e)", b=NB),
+            in_=freq_cis.rearrange("(b p) i e -> p b (i e)", p=P),
+        )
+
+        make_identity(nc, ident[:])
+        nc.vector.memset(ones[:], 1.0)
+        nc.vector.memset(eps[:], 1e-6)
+        nc.scalar.activation(dummy[:], eps[:], ACT.Abs_reciprocal_sqrt)
+        nc.gpsimd.tensor_scalar(ss[:, :, 0:1], fr[:, :, 1:2], 1.0, 0.0, ALU.mult, ALU.add)
+        nc.gpsimd.tensor_scalar(ss[:, :, 1:2], fr[:, :, 1:2], -1.0, 0.0, ALU.mult, ALU.add)
+
+        wg = {}
+        xg = {}
+        wide = {}
+        dg = {}
+        tp = {}
+        lat = {}
+        ng = {}
+        nb = {}
+        kr = psum.tile([P, NB, P], F32, name="kr")
+        idle = list(range(7))
+
+        def take():
+            i = idle[0]
+            idle.remove(i)
+            return i, psum.tile([P, 512], F32, name="bank%d" % i)
+
+
+        def w_inter_v(g):
+            wg[g] = work.tile([P, WIDTH, 4], BF16, name="wg", align_bytes=64)
+            nc.vector.tensor_copy(wg[g][:, 0:SPLIT, :], wraw[g][:, :, 0:SPLIT].rearrange("p j w -> p w j"))
+
+        def w_inter_s(g):
+            nc.scalar.copy(wg[g][:, SPLIT:WIDTH, :], wraw[g][:, :, SPLIT:WIDTH].rearrange("p j w -> p w j"))
+
+        def w_quant(g):
+            flat = wg[g][:].rearrange("p w j -> p (w j)")
+            nc.vector.quantize_mx(out=wc[g][:, 0:LORA].bitcast(FP8X4), scales=ws[g][:, 0:LORA], in_=flat[:, 0 : 4 * LORA])
+            nc.vector.quantize_mx(out=wc[g][:, LORA:WIDTH].bitcast(FP8X4), scales=ws[g][:, LORA:WIDTH], in_=flat[:, 4 * LORA : 4 * WIDTH])
+
+        def x_trans(b):
+            words = xraw[b][:].bitcast(F32)
+            for h in range(2):
+                tp[(b, h)] = take()
+                t = tp[(b, h)][1][:].rearrange("p (a r) -> p a r", a=4)
+                for gg in range(2):
+                    for u in range(2):
+                        nc.tensor.transpose(t[:, 2 * gg + u, :], words[:, 256 * (2 * h + gg) + u : 256 * (2 * h + gg + 1) : 2], ident[:])
+
+        def x_out(b):
+            xg[b] = work.tile([P, NP, P, 4], BF16, name="xg", align_bytes=64)
+            flat = xg[b][:].rearrange("p g r t -> p (g r t)").bitcast(F32)
+            for h in range(2):
+                i, t = tp[(b, h)]
+                nc.scalar.copy(
+                    flat[:, 512 * h : 512 * (h + 1)].rearrange("p (g r u) -> p g r u", g=2, u=2),
+                    t[:].rearrange("p (g u r) -> p g r u", g=2, u=2),
+                )
+                idle.append(i)
+
+        def x_quant(b):
+            nc.vector.quantize_mx(
+                out=xc[b][:].rearrange("p g r -> p (g r)").bitcast(FP8X4),
+                scales=xs[b][:].rearrange("p g r -> p (g r)"),
+                in_=xg[b][:].rearrange("p g r t -> p (g r t)"),
+            )
+
+        def lat_pass(b, g):
+            if g == 0:
+                lat[b] = take()
+            nc.tensor.matmul_mx(
+                out=lat[b][1][:],
+                lhsT=xc[b][:, g, :].bitcast(FP8X4),
+                lhsT_scale=xs[b][:, g, :],
+                rhs=wc[g][:, 0:LORA].bitcast(FP8X4),
+                rhs_scale=ws[g][:, 0:LORA],
+                start=(g == 0),
+                stop=(g == NP - 1),
+            )
+
+        def kr_passes(b):
+            for g in range(NP):
+                nc.tensor.matmul_mx(
+                    out=kr[:, b, :],
+                    lhsT=xc[b][:, g, :].bitcast(FP8X4),
+                    lhsT_scale=xs[b][:, g, :],
+                    rhs=wc[g][:, LORA:WIDTH].bitcast(FP8X4),
+                    rhs_scale=ws[g][:, LORA:WIDTH],
+                    start=(g == 0),
+                    stop=(g == NP - 1),
+                )
+
+        def stats(b):
+            sq = work.tile([P, LORA], BF16, name="sq")
+            nc.scalar.activation(sq[:], lat[b][1][:], ACT.Square, accum_out=sumsq[b][:])
+
+        def root(b):
+            nc.scalar.activation(rstd[b][:], sumsq[b][:], ACT.Abs_reciprocal_sqrt, bias=eps[:], scale=1.0 / LORA)
+
+        def norm(b):
+            nb[b] = work.tile([P, LORA], BF16, name="nb")
+            nc.vector.scalar_tensor_tensor(nb[b][:], lat[b][1][:], rstd[b][:], gain[:], ALU.mult, ALU.mult)
+            idle.append(lat[b][0])
+
+        def n_trans(b):
+            tp[(b, 2)] = take()
+            words = nb[b][:].bitcast(F32)
+            for u in range(2):
+                nc.tensor.transpose(tp[(b, 2)][1][:, P * u : P * (u + 1)], words[:, u::2], ident[:])
+
+        def n_out(b):
+            ng[b] = work.tile([P, P, 4], BF16, name="ng", align_bytes=64)
+            i, t = tp[(b, 2)]
+            nc.scalar.copy(
+                ng[b][:].rearrange("p r t -> p (r t)").bitcast(F32).rearrange("p (r u) -> p r u", u=2),
+                t[:, 0 : 2 * P].rearrange("p (u r) -> p r u", u=2),
+            )
+            idle.append(i)
+
+        def n_quant(b):
+            nc.vector.quantize_mx(out=ncod[b][:].bitcast(FP8X4), scales=nsc[b][:], in_=ng[b][:].rearrange("p r t -> p (r t)"))
+
+        def bytes_of(c):
+            o, n = CHUNKS[c]
+            for i, (bo, bn) in enumerate(BLOADS):
+                if bo <= o < bo + bn:
+                    return wb[i], o - bo, n
+
+        def widen_s(c):
+            t, o, n = bytes_of(c)
+            wide[c] = work.tile([P, 4, n], BF16, name="wide", bufs=4)
+            for j in range(4 - APL[c], 4):
+                nc.scalar.activation(wide[c][:, j, :], t[:, j, o : o + n].bitcast(FP8), ACT.Copy, scale=scale[:, j : j + 1])
+
+        def widen_v(c):
+            t, o, n = bytes_of(c)
+            for j in range(4 - APL[c]):
+                nc.vector.tensor_scalar(wide[c][:, j, :], t[:, j, o : o + n].bitcast(FP8), scale[:, j : j + 1], None, ALU.mult)
+
+        def d_inter(c):
+            dg[c] = work.tile([P, CHUNKS[c][1], 4], BF16, name="dg", align_bytes=64)
+            nc.vector.tensor_copy(dg[c][:], wide[c][:].rearrange("p j w -> p w j"))
+
+        def d_quant(c):
+            nc.vector.quantize_mx(out=dc[c][:].bitcast(FP8X4), scales=ds[c][:], in_=dg[c][:].rearrange("p w j -> p (w j)"))
+
+        def kv(b, c, eng="s"):
+            o0, n = CHUNKS[c]
+            i, bank = take()
+            acc = bank[:, 0:n]
+            idle.append(i)
+            nc.tensor.matmul_mx(
+                out=acc,
+                lhsT=ncod[b][:].bitcast(FP8X4),
+                lhsT_scale=nsc[b][:],
+                rhs=dc[c][:].bitcast(FP8X4),
+                rhs_scale=ds[c][:],
+                start=True,
+                stop=True,
+            )
+            o = outs.tile([P, n], F32, name="o")
+            if eng == "s":
+                nc.scalar.copy(o[:], acc)
+            else:
+                nc.vector.tensor_copy(o[:], acc)
+            nc.sync.dma_start(out=kvf[b * P : (b + 1) * P, o0 : o0 + n], in_=o[:])
+
+        def rope():
+            k2 = kr[:].rearrange("p b (i e) -> p (b i) e", e=2)
+            t1 = work.tile([P, NB * 64, 2], F32, name="t1")
+            t2 = work.tile([P, NB * 64, 2], F32, name="t2")
+            ro = work.tile([P, NB * 64, 2], F32, name="ro")
+            nc.vector.tensor_tensor(t1[:], k2, fr[:, :, 0:1].to_broadcast([P, NB * 64, 2]), ALU.mult)
+            nc.vector.tensor_tensor(t2[:], k2, ss[:], ALU.mult)
+            nc.vector.tensor_tensor(ro[:], t1[:], t2[:, :, ::-1], ALU.add)
+            nc.sync.dma_start(
+                out=krf.rearrange("(b p) f -> p b f", p=P),
+                in_=ro[:].rearrange("p (b i) e -> p b (i e)", b=NB),
+            )
+
+        def gains():
+            i, t = take()
+            nc.tensor.matmul(t[:], lhsT=ones[:], rhs=grow[:], start=True, stop=True)
+            nc.scalar.copy(gain[:], t[:])
+            idle.append(i)
+
+        def lats(b):
+            for g in range(NP):
+                lat_pass(b, g)
+            kr_passes(b)
+
+        gains(); w_inter_v(0); w_inter_s(0); w_quant(0); x_trans(0); w_inter_v(1); w_inter_s(1); w_inter_v(2)
+        w_inter_s(2); w_inter_v(3); w_inter_s(3); w_quant(1); x_out(0); w_quant(2); widen_s(0); w_quant(3); x_trans(1)
+        x_out(1); widen_s(1); x_trans(2); x_out(2); x_trans(3); x_quant(0); lat_pass(0, 0); widen_s(2); widen_v(0)
+        lat_pass(0, 1); widen_v(1); x_quant(1); lat_pass(0, 2); d_inter(0); lat_pass(0, 3); x_quant(2); lat_pass(2, 0)
+        d_inter(1); lat_pass(2, 1); x_out(3); widen_s(3); stats(0); lat_pass(1, 0); lat_pass(1, 1); lat_pass(2, 2)
+        widen_v(2); x_quant(3); lat_pass(1, 2); lat_pass(2, 3); widen_s(5); lat_pass(1, 3); stats(1); lat_pass(3, 0)
+        widen_v(3); lat_pass(3, 1); kr_passes(3); kr_passes(0); root(0); stats(2); norm(0); n_trans(0); root(1)
+        norm(1); lat_pass(3, 2); d_inter(2); n_out(0); widen_s(4); root(2); norm(2); d_quant(1); n_trans(1); n_out(1)
+        n_quant(1); lat_pass(3, 3); n_quant(0); d_quant(0); widen_s(6); stats(3); root(3); n_trans(2); norm(3)
+        n_out(2); n_quant(2); kv(1, 1); kv(0, 1); d_quant(2); kv(1, 0); n_trans(3); n_out(3); d_inter(3); kv(0, 0)
+        kv(1, 2); kv(2, 0); n_quant(3); d_quant(3); kv(3, 1); kv(2, 1); kv(3, 2); kv(0, 2); kv(2, 2); kv(3, 0)
+        kr_passes(2); widen_s(7); widen_v(5); widen_v(4); kv(2, 3); kv(1, 3); kv(3, 3); d_inter(5); d_inter(4)
+        kv(0, 3); d_quant(5); d_quant(4); widen_v(6); kv(3, 5); kv(0, 4); kv(2, 4); kv(3, 4); kv(0, 5); kv(2, 5)
+        kv(1, 4); d_inter(6); d_quant(6); kv(1, 5); kv(2, 6); widen_v(7); widen_s(8); d_inter(7); kv(1, 6); kv(0, 6)
+        d_quant(7); kv(1, 7); widen_v(8); d_inter(8); kv(3, 6); kr_passes(1); kv(0, 7); kv(2, 7); d_quant(8); kv(0, 8)
+        rope(); kv(1, 8, "v"); kv(3, 7); kv(2, 8); kv(3, 8, "v")

@@ -23,7 +23,8 @@ APL = [1, 1, 1, 1, 1, 1, 1, 1, 1]
 CHUNKS = [(512 * c, 512) for c in range(7)] + [(3584, 256), (3840, 256)]
 NCH = len(CHUNKS)
 BLOADS = [(0, 512), (512, 512), (1024, 1024), (2048, 2048)]
-SPLIT = 448
+SPLIT = 512
+WENG = "sv"
 
 
 def tile_multiheadlatentattention_pa_kernel(tc, x, freq_cis, Wckv, kv_norm_w, Wdkv_bytes, Wdkv_scale, out_0, out_1):
@@ -40,6 +41,7 @@ def tile_multiheadlatentattention_pa_kernel(tc, x, freq_cis, Wckv, kv_norm_w, Wd
         ctx.enter_context(tc.manual_schedule())
 
         ident = keep.tile([P, P], F32, name="ident")
+        identb = keep.tile([P, P], BF16, name="identb")
         ones = keep.tile([P, P], BF16, name="ones")
         grow = keep.tile([P, LORA], BF16, name="grow")
         gain = keep.tile([P, LORA], F32, name="gain")
@@ -72,19 +74,21 @@ def tile_multiheadlatentattention_pa_kernel(tc, x, freq_cis, Wckv, kv_norm_w, Wd
             nc.sync.dma_start(out=wraw[g][:], in_=wv[g])
 
         nc.vector.memset(grow[:], 0.0)
-        nc.scalar.dma_start(out=grow[0:1, :], in_=kv_norm_w.rearrange("(o n) -> o n", o=1))
-        nc.scalar.dma_start(out=scale[:], in_=Wdkv_scale.rearrange("(p j) o -> p (j o)", j=4))
         def load_b(c):
             o, n = BLOADS[c]
             nc.sync.dma_start(out=wb[c][:], in_=bv[:, :, o : o + n])
 
-        for g in range(NP):
-            load_w(g)
-        load_x(0)
-        load_x(1)
+        nc.sync.dma_start(out=scale[:], in_=Wdkv_scale.rearrange("(p j) o -> p (j o)", j=4))
         load_b(0)
-        load_x(2)
+        load_w(0)
+        load_w(1)
+        load_w(2)
+        nc.scalar.dma_start(out=grow[0:1, :], in_=kv_norm_w.rearrange("(o n) -> o n", o=1))
+        load_x(0)
+        load_w(3)
+        load_x(1)
         load_b(1)
+        load_x(2)
         load_x(3)
         load_b(2)
         load_b(3)
@@ -93,6 +97,7 @@ def tile_multiheadlatentattention_pa_kernel(tc, x, freq_cis, Wckv, kv_norm_w, Wd
             in_=freq_cis.rearrange("(b p) i e -> p b (i e)", p=P),
         )
 
+        make_identity(nc, identb[:])
         make_identity(nc, ident[:])
         nc.vector.memset(ones[:], 1.0)
         nc.vector.memset(eps[:], 1e-6)
@@ -117,12 +122,35 @@ def tile_multiheadlatentattention_pa_kernel(tc, x, freq_cis, Wckv, kv_norm_w, Wd
             return i, psum.tile([P, 512], F32, name="bank%d" % i)
 
 
-        def w_inter_v(g):
-            wg[g] = work.tile([P, WIDTH, 4], BF16, name="wg", align_bytes=64)
-            nc.vector.tensor_copy(wg[g][:, 0:SPLIT, :], wraw[g][:, :, 0:SPLIT].rearrange("p j w -> p w j"))
+        def w_pe(g, h):
+            i, t = take()
+            tp[("w", g, h)] = (i, t)
+            for q in range(2):
+                c0 = 256 * h + 128 * q
+                nc.tensor.matmul(
+                    t[:].bitcast(BF16)[:, 512 * q : 512 * (q + 1)],
+                    lhsT=identb[:],
+                    rhs=wraw[g][:, :, c0 : c0 + 128].rearrange("p j w -> p w j"),
+                    start=True,
+                    stop=True,
+                )
+
+        def w_out(g, h):
+            i, t = tp[("w", g, h)]
+            o = wg_tile(g)[:].rearrange("p w j -> p (w j)")[:, 1024 * h : 1024 * (h + 1)]
+            if WENG[h] == "s":
+                nc.scalar.copy(o, t[:].bitcast(BF16))
+            else:
+                nc.vector.tensor_copy(o, t[:].bitcast(BF16))
+            idle.append(i)
+
+        def wg_tile(g):
+            if g not in wg:
+                wg[g] = work.tile([P, WIDTH, 4], BF16, name="wg", align_bytes=64)
+            return wg[g]
 
         def w_inter_s(g):
-            nc.scalar.copy(wg[g][:, SPLIT:WIDTH, :], wraw[g][:, :, SPLIT:WIDTH].rearrange("p j w -> p w j"))
+            nc.scalar.copy(wg_tile(g)[:, SPLIT:WIDTH, :], wraw[g][:, :, SPLIT:WIDTH].rearrange("p j w -> p w j"))
 
         def w_quant(g):
             flat = wg[g][:].rearrange("p w j -> p (w j)")
@@ -217,16 +245,20 @@ def tile_multiheadlatentattention_pa_kernel(tc, x, freq_cis, Wckv, kv_norm_w, Wd
                 if bo <= o < bo + bn:
                     return wb[i], o - bo, n
 
+        def wide_tile(c):
+            if c not in wide:
+                wide[c] = work.tile([P, 4, CHUNKS[c][1]], BF16, name="wide", bufs=4)
+            return wide[c]
+
         def widen_s(c):
             t, o, n = bytes_of(c)
-            wide[c] = work.tile([P, 4, n], BF16, name="wide", bufs=4)
             for j in range(4 - APL[c], 4):
-                nc.scalar.activation(wide[c][:, j, :], t[:, j, o : o + n].bitcast(FP8), ACT.Copy, scale=scale[:, j : j + 1])
+                nc.scalar.activation(wide_tile(c)[:, j, :], t[:, j, o : o + n].bitcast(FP8), ACT.Copy, scale=scale[:, j : j + 1])
 
         def widen_v(c):
             t, o, n = bytes_of(c)
             for j in range(4 - APL[c]):
-                nc.vector.tensor_scalar(wide[c][:, j, :], t[:, j, o : o + n].bitcast(FP8), scale[:, j : j + 1], None, ALU.mult)
+                nc.vector.tensor_scalar(wide_tile(c)[:, j, :], t[:, j, o : o + n].bitcast(FP8), scale[:, j : j + 1], None, ALU.mult)
 
         def d_inter(c):
             dg[c] = work.tile([P, CHUNKS[c][1], 4], BF16, name="dg", align_bytes=64)
@@ -235,13 +267,11 @@ def tile_multiheadlatentattention_pa_kernel(tc, x, freq_cis, Wckv, kv_norm_w, Wd
         def d_quant(c):
             nc.vector.quantize_mx(out=dc[c][:].bitcast(FP8X4), scales=ds[c][:], in_=dg[c][:].rearrange("p w j -> p (w j)"))
 
-        def kv(b, c, eng="s"):
-            o0, n = CHUNKS[c]
-            i, bank = take()
-            acc = bank[:, 0:n]
-            idle.append(i)
+        def kv_mm(b, c):
+            n = CHUNKS[c][1]
+            tp[("kv", b, c)] = take()
             nc.tensor.matmul_mx(
-                out=acc,
+                out=tp[("kv", b, c)][1][:, 0:n],
                 lhsT=ncod[b][:].bitcast(FP8X4),
                 lhsT_scale=nsc[b][:],
                 rhs=dc[c][:].bitcast(FP8X4),
@@ -249,11 +279,16 @@ def tile_multiheadlatentattention_pa_kernel(tc, x, freq_cis, Wckv, kv_norm_w, Wd
                 start=True,
                 stop=True,
             )
+
+        def kv_out(b, c, eng="s"):
+            o0, n = CHUNKS[c]
+            i, t = tp[("kv", b, c)]
             o = outs.tile([P, n], F32, name="o")
             if eng == "s":
-                nc.scalar.copy(o[:], acc)
+                nc.scalar.copy(o[:], t[:, 0:n])
             else:
-                nc.vector.tensor_copy(o[:], acc)
+                nc.vector.tensor_copy(o[:], t[:, 0:n])
+            idle.append(i)
             nc.sync.dma_start(out=kvf[b * P : (b + 1) * P, o0 : o0 + n], in_=o[:])
 
         def rope():
@@ -280,19 +315,26 @@ def tile_multiheadlatentattention_pa_kernel(tc, x, freq_cis, Wckv, kv_norm_w, Wd
                 lat_pass(b, g)
             kr_passes(b)
 
-        gains(); w_inter_v(0); w_inter_s(0); w_quant(0); x_trans(0); w_inter_v(1); w_inter_s(1); w_inter_v(2)
-        w_inter_s(2); w_inter_v(3); w_inter_s(3); w_quant(1); x_out(0); w_quant(2); widen_s(0); w_quant(3); x_trans(1)
-        x_out(1); widen_s(1); x_trans(2); x_out(2); x_trans(3); x_quant(0); lat_pass(0, 0); widen_s(2); widen_v(0)
-        lat_pass(0, 1); widen_v(1); x_quant(1); lat_pass(0, 2); d_inter(0); lat_pass(0, 3); x_quant(2); lat_pass(2, 0)
-        d_inter(1); lat_pass(2, 1); x_out(3); widen_s(3); stats(0); lat_pass(1, 0); lat_pass(1, 1); lat_pass(2, 2)
-        widen_v(2); x_quant(3); lat_pass(1, 2); lat_pass(2, 3); widen_s(5); lat_pass(1, 3); stats(1); lat_pass(3, 0)
-        widen_v(3); lat_pass(3, 1); kr_passes(3); kr_passes(0); root(0); stats(2); norm(0); n_trans(0); root(1)
-        norm(1); lat_pass(3, 2); d_inter(2); n_out(0); widen_s(4); root(2); norm(2); d_quant(1); n_trans(1); n_out(1)
-        n_quant(1); lat_pass(3, 3); n_quant(0); d_quant(0); widen_s(6); stats(3); root(3); n_trans(2); norm(3)
-        n_out(2); n_quant(2); kv(1, 1); kv(0, 1); d_quant(2); kv(1, 0); n_trans(3); n_out(3); d_inter(3); kv(0, 0)
-        kv(1, 2); kv(2, 0); n_quant(3); d_quant(3); kv(3, 1); kv(2, 1); kv(3, 2); kv(0, 2); kv(2, 2); kv(3, 0)
-        kr_passes(2); widen_s(7); widen_v(5); widen_v(4); kv(2, 3); kv(1, 3); kv(3, 3); d_inter(5); d_inter(4)
-        kv(0, 3); d_quant(5); d_quant(4); widen_v(6); kv(3, 5); kv(0, 4); kv(2, 4); kv(3, 4); kv(0, 5); kv(2, 5)
-        kv(1, 4); d_inter(6); d_quant(6); kv(1, 5); kv(2, 6); widen_v(7); widen_s(8); d_inter(7); kv(1, 6); kv(0, 6)
-        d_quant(7); kv(1, 7); widen_v(8); d_inter(8); kv(3, 6); kr_passes(1); kv(0, 7); kv(2, 7); d_quant(8); kv(0, 8)
-        rope(); kv(1, 8, "v"); kv(3, 7); kv(2, 8); kv(3, 8, "v")
+        w_pe(0, 0); widen_v(0); w_pe(0, 1); widen_s(0); w_inter_s(0); w_pe(1, 0); d_inter(0); d_quant(0); w_inter_s(1)
+        w_out(0, 1); w_out(0, 0); w_quant(0); w_pe(1, 1); w_out(1, 1); w_inter_s(2); w_out(1, 0); w_quant(1); gains()
+        w_pe(2, 0); w_pe(2, 1); w_out(2, 0); w_out(2, 1); w_quant(2); x_trans(0); x_out(0); w_pe(3, 1); w_inter_s(3)
+        w_pe(3, 0); x_quant(0); w_out(3, 0); widen_v(1); x_trans(1); x_trans(2); x_out(1); w_out(3, 1); w_quant(3)
+        x_trans(3); lat_pass(0, 0); lat_pass(0, 1); x_out(2); x_quant(1); lat_pass(0, 2); lat_pass(1, 0); x_out(3)
+        x_quant(2); widen_v(3); lat_pass(2, 0); x_quant(3); lat_pass(2, 1); lat_pass(0, 3); kr_passes(0); lat_pass(2, 2); lat_pass(2, 3)
+        lat_pass(1, 1); widen_s(3); d_inter(3); widen_s(2); widen_s(1); lat_pass(3, 0); widen_s(4); stats(2); d_inter(1)
+        lat_pass(1, 2); lat_pass(3, 1); lat_pass(3, 2); lat_pass(3, 3); stats(0); root(2); norm(2); root(0); norm(0)
+        stats(3); lat_pass(1, 3); n_trans(2); d_quant(3); stats(1); root(3); widen_v(2); n_out(2); n_quant(2)
+        root(1); norm(1); kr_passes(1); n_trans(0); widen_s(5); kv_mm(2, 3); n_out(0); widen_s(6); kv_out(2, 3)
+        d_quant(1); norm(3); n_trans(1); n_out(1); kv_mm(2, 1); kv_out(2, 1); kv_mm(2, 0); kv_out(2, 0); n_quant(0)
+        kv_mm(0, 3); kv_out(0, 3); n_quant(1); kv_mm(1, 0); d_inter(2); n_trans(3); n_out(3); kv_mm(0, 1); widen_v(4)
+        kv_out(0, 1); kv_mm(1, 1); n_quant(3); kv_out(1, 0); kv_mm(3, 1); d_quant(2); kv_out(1, 1); kv_out(3, 1)
+        d_inter(4); kv_mm(3, 3); kv_out(3, 3); kv_mm(3, 0); kv_mm(0, 0); kv_out(0, 0); widen_v(5); d_quant(4)
+        d_inter(5); kv_mm(1, 3); widen_v(8); kv_out(1, 3); kv_mm(2, 2); kv_mm(1, 2); kr_passes(3); kv_mm(3, 2)
+        kv_out(3, 2); kv_out(3, 0); widen_s(8); kv_mm(0, 4); kv_out(0, 4); d_quant(5); kv_mm(0, 2); kv_out(0, 2)
+        kv_mm(2, 4); kv_mm(1, 4); kv_mm(2, 5); kv_mm(0, 5); d_inter(8); kv_mm(1, 5); d_quant(8); kv_out(1, 4)
+        kv_mm(3, 4); kv_out(2, 4); kv_mm(2, 8); kv_out(2, 5); widen_v(6); d_inter(6); kv_out(0, 5); kv_mm(0, 8)
+        kr_passes(2); kv_out(3, 4); kv_mm(3, 5); kv_mm(3, 8); kv_out(1, 2); kv_out(3, 5); kv_out(1, 5); kv_out(2, 2)
+        d_quant(6); kv_mm(3, 6); widen_s(7); widen_v(7); kv_mm(1, 6); d_inter(7); kv_out(2, 8); kv_out(0, 8); kv_mm(0, 6)
+        kv_out(0, 6); kv_mm(1, 8); kv_mm(2, 6); kv_out(2, 6); d_quant(7); kv_out(1, 6); kv_mm(0, 7); kv_out(0, 7)
+        kv_mm(1, 7); kv_out(1, 7); kv_out(3, 8, "v"); kv_mm(3, 7); kv_out(3, 7); rope(); kv_out(1, 8, "v"); kv_out(3, 6)
+        kv_mm(2, 7); kv_out(2, 7)

@@ -19,12 +19,10 @@ ACT = mybir.ActivationFunctionType
 P = 128
 NB = T // P
 NP = C // 512
-APL = [1, 1, 1, 1, 1, 1, 1, 1, 1]
 CHUNKS = [(512 * c, 512) for c in range(7)] + [(3584, 256), (3840, 256)]
 NCH = len(CHUNKS)
 BLOADS = [(0, 512), (512, 512), (1024, 1024), (2048, 2048)]
-SPLIT = 512
-WENG = "sv"
+SPLIT = 448
 
 
 def tile_multiheadlatentattention_pa_kernel(tc, x, freq_cis, Wckv, kv_norm_w, Wdkv_bytes, Wdkv_scale, out_0, out_1):
@@ -41,7 +39,6 @@ def tile_multiheadlatentattention_pa_kernel(tc, x, freq_cis, Wckv, kv_norm_w, Wd
         ctx.enter_context(tc.manual_schedule())
 
         ident = keep.tile([P, P], F32, name="ident")
-        identb = keep.tile([P, P], BF16, name="identb")
         ones = keep.tile([P, P], BF16, name="ones")
         grow = keep.tile([P, LORA], BF16, name="grow")
         gain = keep.tile([P, LORA], F32, name="gain")
@@ -83,9 +80,9 @@ def tile_multiheadlatentattention_pa_kernel(tc, x, freq_cis, Wckv, kv_norm_w, Wd
         load_w(0)
         load_w(1)
         load_w(2)
-        nc.scalar.dma_start(out=grow[0:1, :], in_=kv_norm_w.rearrange("(o n) -> o n", o=1))
         load_x(0)
         load_w(3)
+        nc.scalar.dma_start(out=grow[0:1, :], in_=kv_norm_w.rearrange("(o n) -> o n", o=1))
         load_x(1)
         load_b(1)
         load_x(2)
@@ -97,13 +94,18 @@ def tile_multiheadlatentattention_pa_kernel(tc, x, freq_cis, Wckv, kv_norm_w, Wd
             in_=freq_cis.rearrange("(b p) i e -> p b (i e)", p=P),
         )
 
-        make_identity(nc, identb[:])
         make_identity(nc, ident[:])
         nc.vector.memset(ones[:], 1.0)
         nc.vector.memset(eps[:], 1e-6)
         nc.scalar.activation(dummy[:], eps[:], ACT.Abs_reciprocal_sqrt)
         nc.gpsimd.tensor_scalar(ss[:, :, 0:1], fr[:, :, 1:2], 1.0, 0.0, ALU.mult, ALU.add)
         nc.gpsimd.tensor_scalar(ss[:, :, 1:2], fr[:, :, 1:2], -1.0, 0.0, ALU.mult, ALU.add)
+
+        def four(t):
+            return t.rearrange("p (c i) t -> p c t i", i=4)
+
+        def by_four(t):
+            return t.rearrange("p t (c i) -> p c t i", i=4)
 
         wg = {}
         xg = {}
@@ -122,60 +124,47 @@ def tile_multiheadlatentattention_pa_kernel(tc, x, freq_cis, Wckv, kv_norm_w, Wd
             return i, psum.tile([P, 512], F32, name="bank%d" % i)
 
 
-        def w_pe(g, h):
-            i, t = take()
-            tp[("w", g, h)] = (i, t)
-            for q in range(2):
-                c0 = 256 * h + 128 * q
-                nc.tensor.matmul(
-                    t[:].bitcast(BF16)[:, 512 * q : 512 * (q + 1)],
-                    lhsT=identb[:],
-                    rhs=wraw[g][:, :, c0 : c0 + 128].rearrange("p j w -> p w j"),
-                    start=True,
-                    stop=True,
-                )
-
-        def w_out(g, h):
-            i, t = tp[("w", g, h)]
-            o = wg_tile(g)[:].rearrange("p w j -> p (w j)")[:, 1024 * h : 1024 * (h + 1)]
-            if WENG[h] == "s":
-                nc.scalar.copy(o, t[:].bitcast(BF16))
-            else:
-                nc.vector.tensor_copy(o, t[:].bitcast(BF16))
-            idle.append(i)
-
         def wg_tile(g):
             if g not in wg:
                 wg[g] = work.tile([P, WIDTH, 4], BF16, name="wg", align_bytes=64)
             return wg[g]
 
+        def w_inter_v(g):
+            nc.vector.tensor_copy(four(wg_tile(g)[:, 0:SPLIT, :]), by_four(wraw[g][:, :, 0:SPLIT]))
+
         def w_inter_s(g):
-            nc.scalar.copy(wg_tile(g)[:, SPLIT:WIDTH, :], wraw[g][:, :, SPLIT:WIDTH].rearrange("p j w -> p w j"))
+            nc.scalar.copy(four(wg_tile(g)[:, SPLIT:WIDTH, :]), by_four(wraw[g][:, :, SPLIT:WIDTH]))
 
         def w_quant(g):
             flat = wg[g][:].rearrange("p w j -> p (w j)")
             nc.vector.quantize_mx(out=wc[g][:, 0:LORA].bitcast(FP8X4), scales=ws[g][:, 0:LORA], in_=flat[:, 0 : 4 * LORA])
             nc.vector.quantize_mx(out=wc[g][:, LORA:WIDTH].bitcast(FP8X4), scales=ws[g][:, LORA:WIDTH], in_=flat[:, 4 * LORA : 4 * WIDTH])
 
-        def x_trans(b):
+        def x_trans(b, h):
             words = xraw[b][:].bitcast(F32)
-            for h in range(2):
-                tp[(b, h)] = take()
-                t = tp[(b, h)][1][:].rearrange("p (a r) -> p a r", a=4)
-                for gg in range(2):
-                    for u in range(2):
-                        nc.tensor.transpose(t[:, 2 * gg + u, :], words[:, 256 * (2 * h + gg) + u : 256 * (2 * h + gg + 1) : 2], ident[:])
+            tp[(b, h)] = take()
+            t = tp[(b, h)][1][:].rearrange("p (a r) -> p a r", a=4)
+            for gg in range(2):
+                for u in range(2):
+                    nc.tensor.transpose(t[:, 2 * gg + u, :], words[:, 256 * (2 * h + gg) + u : 256 * (2 * h + gg + 1) : 2], ident[:])
 
-        def x_out(b):
-            xg[b] = work.tile([P, NP, P, 4], BF16, name="xg", align_bytes=64)
+        def copy(eng, out, in_):
+            if eng == "v":
+                nc.vector.tensor_copy(out, in_)
+            else:
+                nc.scalar.copy(out, in_)
+
+        def x_out(b, h, eng):
+            if b not in xg:
+                xg[b] = work.tile([P, NP, P, 4], BF16, name="xg", align_bytes=64)
             flat = xg[b][:].rearrange("p g r t -> p (g r t)").bitcast(F32)
-            for h in range(2):
-                i, t = tp[(b, h)]
-                nc.scalar.copy(
-                    flat[:, 512 * h : 512 * (h + 1)].rearrange("p (g r u) -> p g r u", g=2, u=2),
-                    t[:].rearrange("p (g u r) -> p g r u", g=2, u=2),
-                )
-                idle.append(i)
+            i, t = tp[(b, h)]
+            copy(
+                eng,
+                flat[:, 512 * h : 512 * (h + 1)].rearrange("p (g r u) -> p g r u", g=2, u=2),
+                t[:].rearrange("p (g u r) -> p g r u", g=2, u=2),
+            )
+            idle.append(i)
 
         def x_quant(b):
             nc.vector.quantize_mx(
@@ -245,24 +234,20 @@ def tile_multiheadlatentattention_pa_kernel(tc, x, freq_cis, Wckv, kv_norm_w, Wd
                 if bo <= o < bo + bn:
                     return wb[i], o - bo, n
 
-        def wide_tile(c):
+        def widen(c, j, eng):
+            t, o, n = bytes_of(c)
             if c not in wide:
-                wide[c] = work.tile([P, 4, CHUNKS[c][1]], BF16, name="wide", bufs=4)
-            return wide[c]
-
-        def widen_s(c):
-            t, o, n = bytes_of(c)
-            for j in range(4 - APL[c], 4):
-                nc.scalar.activation(wide_tile(c)[:, j, :], t[:, j, o : o + n].bitcast(FP8), ACT.Copy, scale=scale[:, j : j + 1])
-
-        def widen_v(c):
-            t, o, n = bytes_of(c)
-            for j in range(4 - APL[c]):
-                nc.vector.tensor_scalar(wide_tile(c)[:, j, :], t[:, j, o : o + n].bitcast(FP8), scale[:, j : j + 1], None, ALU.mult)
+                wide[c] = keep.tile([P, 4, n], BF16, name="wide%d" % c)
+            w = wide[c][:, j, :]
+            b = t[:, j, o : o + n].bitcast(FP8)
+            if eng == "v":
+                nc.vector.tensor_scalar(w, b, scale[:, j : j + 1], None, ALU.mult)
+            else:
+                nc.scalar.activation(w, b, ACT.Copy, scale=scale[:, j : j + 1])
 
         def d_inter(c):
             dg[c] = work.tile([P, CHUNKS[c][1], 4], BF16, name="dg", align_bytes=64)
-            nc.vector.tensor_copy(dg[c][:], wide[c][:].rearrange("p j w -> p w j"))
+            nc.vector.tensor_copy(four(dg[c][:]), by_four(wide[c][:]))
 
         def d_quant(c):
             nc.vector.quantize_mx(out=dc[c][:].bitcast(FP8X4), scales=ds[c][:], in_=dg[c][:].rearrange("p w j -> p (w j)"))
@@ -280,22 +265,19 @@ def tile_multiheadlatentattention_pa_kernel(tc, x, freq_cis, Wckv, kv_norm_w, Wd
                 stop=True,
             )
 
-        def kv_out(b, c, eng="s"):
+        def kv_out(b, c, eng):
             o0, n = CHUNKS[c]
             i, t = tp[("kv", b, c)]
             o = outs.tile([P, n], F32, name="o")
-            if eng == "s":
-                nc.scalar.copy(o[:], t[:, 0:n])
-            else:
-                nc.vector.tensor_copy(o[:], t[:, 0:n])
+            copy(eng, o[:], t[:, 0:n])
             idle.append(i)
             nc.sync.dma_start(out=kvf[b * P : (b + 1) * P, o0 : o0 + n], in_=o[:])
 
         def rope():
             k2 = kr[:].rearrange("p b (i e) -> p (b i) e", e=2)
-            t1 = work.tile([P, NB * 64, 2], F32, name="t1")
-            t2 = work.tile([P, NB * 64, 2], F32, name="t2")
-            ro = work.tile([P, NB * 64, 2], F32, name="ro")
+            t1 = work.tile([P, NB * 64, 2], F32, name="t1", bufs=1)
+            t2 = work.tile([P, NB * 64, 2], F32, name="t2", bufs=1)
+            ro = work.tile([P, NB * 64, 2], F32, name="ro", bufs=1)
             nc.vector.tensor_tensor(t1[:], k2, fr[:, :, 0:1].to_broadcast([P, NB * 64, 2]), ALU.mult)
             nc.vector.tensor_tensor(t2[:], k2, ss[:], ALU.mult)
             nc.vector.tensor_tensor(ro[:], t1[:], t2[:, :, ::-1], ALU.add)
@@ -305,36 +287,39 @@ def tile_multiheadlatentattention_pa_kernel(tc, x, freq_cis, Wckv, kv_norm_w, Wd
             )
 
         def gains():
-            i, t = take()
-            nc.tensor.matmul(t[:], lhsT=ones[:], rhs=grow[:], start=True, stop=True)
+            tp["gain"] = take()
+            nc.tensor.matmul(tp["gain"][1][:], lhsT=ones[:], rhs=grow[:], start=True, stop=True)
+
+        def gain_out():
+            i, t = tp["gain"]
             nc.scalar.copy(gain[:], t[:])
             idle.append(i)
 
-        def lats(b):
-            for g in range(NP):
-                lat_pass(b, g)
-            kr_passes(b)
-
-        w_pe(0, 0); widen_v(0); w_pe(0, 1); widen_s(0); w_inter_s(0); w_pe(1, 0); d_inter(0); d_quant(0); w_inter_s(1)
-        w_out(0, 1); w_out(0, 0); w_quant(0); w_pe(1, 1); w_out(1, 1); w_inter_s(2); w_out(1, 0); w_quant(1); gains()
-        w_pe(2, 0); w_pe(2, 1); w_out(2, 0); w_out(2, 1); w_quant(2); x_trans(0); x_out(0); w_pe(3, 1); w_inter_s(3)
-        w_pe(3, 0); x_quant(0); w_out(3, 0); widen_v(1); x_trans(1); x_trans(2); x_out(1); w_out(3, 1); w_quant(3)
-        x_trans(3); lat_pass(0, 0); lat_pass(0, 1); x_out(2); x_quant(1); lat_pass(0, 2); lat_pass(1, 0); x_out(3)
-        x_quant(2); widen_v(3); lat_pass(2, 0); x_quant(3); lat_pass(2, 1); lat_pass(0, 3); kr_passes(0); lat_pass(2, 2); lat_pass(2, 3)
-        lat_pass(1, 1); widen_s(3); d_inter(3); widen_s(2); widen_s(1); lat_pass(3, 0); widen_s(4); stats(2); d_inter(1)
-        lat_pass(1, 2); lat_pass(3, 1); lat_pass(3, 2); lat_pass(3, 3); stats(0); root(2); norm(2); root(0); norm(0)
-        stats(3); lat_pass(1, 3); n_trans(2); d_quant(3); stats(1); root(3); widen_v(2); n_out(2); n_quant(2)
-        root(1); norm(1); kr_passes(1); n_trans(0); widen_s(5); kv_mm(2, 3); n_out(0); widen_s(6); kv_out(2, 3)
-        d_quant(1); norm(3); n_trans(1); n_out(1); kv_mm(2, 1); kv_out(2, 1); kv_mm(2, 0); kv_out(2, 0); n_quant(0)
-        kv_mm(0, 3); kv_out(0, 3); n_quant(1); kv_mm(1, 0); d_inter(2); n_trans(3); n_out(3); kv_mm(0, 1); widen_v(4)
-        kv_out(0, 1); kv_mm(1, 1); n_quant(3); kv_out(1, 0); kv_mm(3, 1); d_quant(2); kv_out(1, 1); kv_out(3, 1)
-        d_inter(4); kv_mm(3, 3); kv_out(3, 3); kv_mm(3, 0); kv_mm(0, 0); kv_out(0, 0); widen_v(5); d_quant(4)
-        d_inter(5); kv_mm(1, 3); widen_v(8); kv_out(1, 3); kv_mm(2, 2); kv_mm(1, 2); kr_passes(3); kv_mm(3, 2)
-        kv_out(3, 2); kv_out(3, 0); widen_s(8); kv_mm(0, 4); kv_out(0, 4); d_quant(5); kv_mm(0, 2); kv_out(0, 2)
-        kv_mm(2, 4); kv_mm(1, 4); kv_mm(2, 5); kv_mm(0, 5); d_inter(8); kv_mm(1, 5); d_quant(8); kv_out(1, 4)
-        kv_mm(3, 4); kv_out(2, 4); kv_mm(2, 8); kv_out(2, 5); widen_v(6); d_inter(6); kv_out(0, 5); kv_mm(0, 8)
-        kr_passes(2); kv_out(3, 4); kv_mm(3, 5); kv_mm(3, 8); kv_out(1, 2); kv_out(3, 5); kv_out(1, 5); kv_out(2, 2)
-        d_quant(6); kv_mm(3, 6); widen_s(7); widen_v(7); kv_mm(1, 6); d_inter(7); kv_out(2, 8); kv_out(0, 8); kv_mm(0, 6)
-        kv_out(0, 6); kv_mm(1, 8); kv_mm(2, 6); kv_out(2, 6); d_quant(7); kv_out(1, 6); kv_mm(0, 7); kv_out(0, 7)
-        kv_mm(1, 7); kv_out(1, 7); kv_out(3, 8, "v"); kv_mm(3, 7); kv_out(3, 7); rope(); kv_out(1, 8, "v"); kv_out(3, 6)
-        kv_mm(2, 7); kv_out(2, 7)
+        widen(0, 0, "v"); widen(0, 1, "s"); widen(0, 3, "v"); widen(0, 2, "v"); d_inter(0); w_inter_s(0); w_inter_v(0)
+        w_inter_s(1); d_quant(0); w_inter_v(1); w_inter_s(2); w_inter_v(2); x_trans(0, 0); x_trans(0, 1); w_quant(0)
+        x_out(0, 0, "s"); w_inter_s(3); w_inter_v(3); gains(); x_out(0, 1, "s"); x_trans(1, 0); w_quant(1); gain_out()
+        x_trans(1, 1); w_quant(3); widen(1, 0, "s"); x_out(1, 0, "s"); x_quant(0); x_trans(2, 0); x_out(1, 1, "s")
+        widen(1, 1, "v"); x_trans(2, 1); w_quant(2); x_out(2, 0, "s"); x_trans(3, 1); x_quant(1); x_out(2, 1, "s")
+        widen(1, 3, "v"); x_trans(3, 0); widen(3, 0, "s"); widen(1, 2, "v"); x_quant(2); x_out(3, 1, "s"); kr_passes(1)
+        d_inter(1); x_out(3, 0, "s"); lat_pass(0, 0); lat_pass(0, 1); widen(2, 0, "s"); lat_pass(0, 2); widen(3, 3, "s")
+        lat_pass(0, 3); x_quant(3); kr_passes(2); widen(5, 3, "s"); d_quant(1); lat_pass(1, 0); lat_pass(3, 0)
+        widen(5, 0, "s"); widen(5, 1, "v"); lat_pass(3, 1); widen(6, 2, "v"); stats(0); lat_pass(3, 2); widen(5, 2, "v")
+        lat_pass(3, 3); widen(7, 3, "v"); widen(4, 3, "s"); widen(6, 0, "v"); lat_pass(2, 0); d_inter(5); lat_pass(1, 1)
+        stats(3); kr_passes(3); root(0); widen(4, 0, "s"); kr_passes(0); lat_pass(2, 1); norm(0); root(3); widen(6, 1, "s")
+        lat_pass(2, 2); norm(3); lat_pass(2, 3); widen(7, 2, "s"); widen(4, 1, "s"); n_trans(0); rope(); n_trans(3)
+        stats(2); lat_pass(1, 2); n_out(3); lat_pass(1, 3); root(2); n_out(0); widen(6, 3, "s"); n_quant(3); n_quant(0)
+        stats(1); norm(2); kv_mm(3, 0); kv_mm(0, 0); d_quant(5); kv_out(3, 0, "s"); kv_mm(3, 1); n_trans(2); kv_out(0, 0, "v")
+        root(1); kv_out(3, 1, "s"); kv_mm(0, 5); norm(1); n_out(2); kv_mm(3, 5); kv_mm(0, 1); kv_out(0, 5, "v")
+        kv_out(3, 5, "s"); n_trans(1); n_quant(2); d_inter(6); kv_out(0, 1, "s"); kv_mm(2, 0); n_out(1); kv_mm(2, 5)
+        kv_out(2, 0, "s"); kv_mm(2, 1); n_quant(1); kv_out(2, 5, "s"); widen(2, 3, "v"); kv_mm(1, 1); d_quant(6)
+        kv_out(2, 1, "s"); kv_mm(1, 5); kv_mm(1, 0); widen(2, 2, "v"); kv_out(1, 1, "s"); kv_mm(3, 6); widen(3, 1, "v")
+        kv_mm(0, 6); widen(4, 2, "v"); kv_out(1, 0, "s"); kv_mm(1, 6); widen(8, 3, "v"); widen(7, 0, "v"); kv_mm(2, 6)
+        d_inter(4); kv_out(0, 6, "s"); kv_out(1, 6, "s"); kv_out(2, 6, "s"); widen(8, 2, "v"); widen(3, 2, "v")
+        kv_out(3, 6, "s"); d_quant(4); kv_out(1, 5, "s"); d_inter(3); kv_mm(0, 4); kv_mm(3, 4); kv_out(0, 4, "s")
+        kv_mm(1, 4); kv_mm(2, 4); kv_out(3, 4, "s"); widen(2, 1, "v"); d_quant(3); kv_out(2, 4, "s"); d_inter(2)
+        kv_out(1, 4, "s"); kv_mm(1, 3); kv_mm(3, 3); kv_out(1, 3, "s"); kv_mm(0, 3); kv_mm(2, 3); kv_out(3, 3, "s")
+        widen(8, 0, "v"); widen(7, 1, "v"); d_quant(2); kv_out(2, 3, "s"); d_inter(7); kv_out(0, 3, "s"); kv_mm(0, 2)
+        kv_mm(2, 2); widen(8, 1, "v"); kv_out(0, 2, "s"); kv_mm(3, 2); d_quant(7); kv_mm(1, 2); d_inter(8); kv_out(2, 2, "s")
+        kv_mm(0, 7); kv_mm(3, 7); kv_mm(2, 7); kv_out(0, 7, "s"); kv_out(3, 2, "v"); kv_mm(1, 7); kv_out(3, 7, "v")
+        d_quant(8); kv_out(2, 7, "v"); kv_mm(0, 8); kv_out(1, 7, "v"); kv_mm(1, 8); kv_mm(2, 8); kv_out(1, 2, "v")
+        kv_out(0, 8, "s"); kv_mm(3, 8); kv_out(2, 8, "s"); kv_out(1, 8, "v"); kv_out(3, 8, "v")

@@ -19,10 +19,10 @@ ACT = mybir.ActivationFunctionType
 P = 128
 NB = T // P
 NP = C // 512
-CHUNKS = [(512 * c, 512) for c in range(7)] + [(3584, 256), (3840, 256)]
+CHUNKS = [(512 * c, 512) for c in range(8)]
 NCH = len(CHUNKS)
 BLOADS = [(0, 512), (512, 512), (1024, 1024), (2048, 2048)]
-SPLIT = 448
+SPLIT = 320
 
 
 def tile_multiheadlatentattention_pa_kernel(tc, x, freq_cis, Wckv, kv_norm_w, Wdkv_bytes, Wdkv_scale, out_0, out_1):
@@ -34,7 +34,7 @@ def tile_multiheadlatentattention_pa_kernel(tc, x, freq_cis, Wckv, kv_norm_w, Wd
     with ExitStack() as ctx:
         keep = ctx.enter_context(tc.tile_pool(name="keep", bufs=1))
         work = ctx.enter_context(tc.tile_pool(name="work", bufs=3))
-        outs = ctx.enter_context(tc.tile_pool(name="outs", bufs=12))
+        outs = ctx.enter_context(tc.tile_pool(name="outs", bufs=8))
         psum = ctx.enter_context(tc.psum_pool(name="psum", bufs=1))
         ctx.enter_context(tc.manual_schedule())
 
@@ -76,15 +76,15 @@ def tile_multiheadlatentattention_pa_kernel(tc, x, freq_cis, Wckv, kv_norm_w, Wd
             nc.sync.dma_start(out=wb[c][:], in_=bv[:, :, o : o + n])
 
         nc.sync.dma_start(out=scale[:], in_=Wdkv_scale.rearrange("(p j) o -> p (j o)", j=4))
-        load_b(0)
         load_w(0)
+        load_x(0)
         load_w(1)
         load_w(2)
-        load_x(0)
         load_w(3)
+        load_b(0)
+        load_b(1)
         nc.scalar.dma_start(out=grow[0:1, :], in_=kv_norm_w.rearrange("(o n) -> o n", o=1))
         load_x(1)
-        load_b(1)
         load_x(2)
         load_x(3)
         load_b(2)
@@ -266,12 +266,16 @@ def tile_multiheadlatentattention_pa_kernel(tc, x, freq_cis, Wckv, kv_norm_w, Wd
             )
 
         def kv_out(b, c, eng):
-            o0, n = CHUNKS[c]
             i, t = tp[("kv", b, c)]
-            o = outs.tile([P, n], F32, name="o")
-            copy(eng, o[:], t[:, 0:n])
+            key = ("o", b, c // 2)
+            first = key not in tp
+            if first:
+                tp[key] = outs.tile([P, 1024], F32, name="o")
+            copy(eng, tp[key][:, 512 * (c % 2) : 512 * (c % 2 + 1)], t[:])
             idle.append(i)
-            nc.sync.dma_start(out=kvf[b * P : (b + 1) * P, o0 : o0 + n], in_=o[:])
+            if not first:
+                m = c // 2
+                nc.sync.dma_start(out=kvf[b * P : (b + 1) * P, 1024 * m : 1024 * (m + 1)], in_=tp[key][:])
 
         def rope():
             k2 = kr[:].rearrange("p b (i e) -> p (b i) e", e=2)
@@ -295,31 +299,29 @@ def tile_multiheadlatentattention_pa_kernel(tc, x, freq_cis, Wckv, kv_norm_w, Wd
             nc.scalar.copy(gain[:], t[:])
             idle.append(i)
 
-        widen(0, 0, "v"); widen(0, 1, "s"); widen(0, 3, "v"); widen(0, 2, "v"); d_inter(0); w_inter_s(0); w_inter_v(0)
-        w_inter_s(1); d_quant(0); w_inter_v(1); w_inter_s(2); w_inter_v(2); x_trans(0, 0); x_trans(0, 1); w_quant(0)
-        x_out(0, 0, "s"); w_inter_s(3); w_inter_v(3); gains(); x_out(0, 1, "s"); x_trans(1, 0); w_quant(1); gain_out()
-        x_trans(1, 1); w_quant(3); widen(1, 0, "s"); x_out(1, 0, "s"); x_quant(0); x_trans(2, 0); x_out(1, 1, "s")
-        widen(1, 1, "v"); x_trans(2, 1); w_quant(2); x_out(2, 0, "s"); x_trans(3, 1); x_quant(1); x_out(2, 1, "s")
-        widen(1, 3, "v"); x_trans(3, 0); widen(3, 0, "s"); widen(1, 2, "v"); x_quant(2); x_out(3, 1, "s"); kr_passes(1)
-        d_inter(1); x_out(3, 0, "s"); lat_pass(0, 0); lat_pass(0, 1); widen(2, 0, "s"); lat_pass(0, 2); widen(3, 3, "s")
-        lat_pass(0, 3); x_quant(3); kr_passes(2); widen(5, 3, "s"); d_quant(1); lat_pass(1, 0); lat_pass(3, 0)
-        widen(5, 0, "s"); widen(5, 1, "v"); lat_pass(3, 1); widen(6, 2, "v"); stats(0); lat_pass(3, 2); widen(5, 2, "v")
-        lat_pass(3, 3); widen(7, 3, "v"); widen(4, 3, "s"); widen(6, 0, "v"); lat_pass(2, 0); d_inter(5); lat_pass(1, 1)
-        stats(3); kr_passes(3); root(0); widen(4, 0, "s"); kr_passes(0); lat_pass(2, 1); norm(0); root(3); widen(6, 1, "s")
-        lat_pass(2, 2); norm(3); lat_pass(2, 3); widen(7, 2, "s"); widen(4, 1, "s"); n_trans(0); rope(); n_trans(3)
-        stats(2); lat_pass(1, 2); n_out(3); lat_pass(1, 3); root(2); n_out(0); widen(6, 3, "s"); n_quant(3); n_quant(0)
-        stats(1); norm(2); kv_mm(3, 0); kv_mm(0, 0); d_quant(5); kv_out(3, 0, "s"); kv_mm(3, 1); n_trans(2); kv_out(0, 0, "v")
-        root(1); kv_out(3, 1, "s"); kv_mm(0, 5); norm(1); n_out(2); kv_mm(3, 5); kv_mm(0, 1); kv_out(0, 5, "v")
-        kv_out(3, 5, "s"); n_trans(1); n_quant(2); d_inter(6); kv_out(0, 1, "s"); kv_mm(2, 0); n_out(1); kv_mm(2, 5)
-        kv_out(2, 0, "s"); kv_mm(2, 1); n_quant(1); kv_out(2, 5, "s"); widen(2, 3, "v"); kv_mm(1, 1); d_quant(6)
-        kv_out(2, 1, "s"); kv_mm(1, 5); kv_mm(1, 0); widen(2, 2, "v"); kv_out(1, 1, "s"); kv_mm(3, 6); widen(3, 1, "v")
-        kv_mm(0, 6); widen(4, 2, "v"); kv_out(1, 0, "s"); kv_mm(1, 6); widen(8, 3, "v"); widen(7, 0, "v"); kv_mm(2, 6)
-        d_inter(4); kv_out(0, 6, "s"); kv_out(1, 6, "s"); kv_out(2, 6, "s"); widen(8, 2, "v"); widen(3, 2, "v")
-        kv_out(3, 6, "s"); d_quant(4); kv_out(1, 5, "s"); d_inter(3); kv_mm(0, 4); kv_mm(3, 4); kv_out(0, 4, "s")
-        kv_mm(1, 4); kv_mm(2, 4); kv_out(3, 4, "s"); widen(2, 1, "v"); d_quant(3); kv_out(2, 4, "s"); d_inter(2)
-        kv_out(1, 4, "s"); kv_mm(1, 3); kv_mm(3, 3); kv_out(1, 3, "s"); kv_mm(0, 3); kv_mm(2, 3); kv_out(3, 3, "s")
-        widen(8, 0, "v"); widen(7, 1, "v"); d_quant(2); kv_out(2, 3, "s"); d_inter(7); kv_out(0, 3, "s"); kv_mm(0, 2)
-        kv_mm(2, 2); widen(8, 1, "v"); kv_out(0, 2, "s"); kv_mm(3, 2); d_quant(7); kv_mm(1, 2); d_inter(8); kv_out(2, 2, "s")
-        kv_mm(0, 7); kv_mm(3, 7); kv_mm(2, 7); kv_out(0, 7, "s"); kv_out(3, 2, "v"); kv_mm(1, 7); kv_out(3, 7, "v")
-        d_quant(8); kv_out(2, 7, "v"); kv_mm(0, 8); kv_out(1, 7, "v"); kv_mm(1, 8); kv_mm(2, 8); kv_out(1, 2, "v")
-        kv_out(0, 8, "s"); kv_mm(3, 8); kv_out(2, 8, "s"); kv_out(1, 8, "v"); kv_out(3, 8, "v")
+        w_inter_v(0); w_inter_s(0); x_trans(0, 0); w_quant(0); x_trans(0, 1); x_out(0, 0, "s"); w_inter_v(1); w_inter_s(1)
+        x_out(0, 1, "v"); w_inter_v(2); w_inter_s(2); x_quant(0); w_quant(1); lat_pass(0, 0); w_inter_s(3); w_inter_v(3)
+        lat_pass(0, 1); w_quant(2); gains(); widen(0, 0, "s"); widen(1, 0, "v"); lat_pass(0, 2); widen(1, 2, "v")
+        gain_out(); widen(1, 1, "v"); x_trans(1, 1); w_quant(3); widen(1, 3, "s"); x_trans(1, 0); x_out(1, 1, "s")
+        widen(0, 3, "v"); x_trans(2, 1); d_inter(1); x_out(1, 0, "s"); lat_pass(0, 3); widen(0, 2, "s"); x_trans(3, 1)
+        stats(0); x_quant(1); widen(0, 1, "s"); d_quant(1); lat_pass(1, 0); root(0); widen(2, 0, "v"); x_out(3, 1, "s")
+        norm(0); lat_pass(1, 1); widen(2, 2, "s"); lat_pass(1, 2); d_inter(0); lat_pass(1, 3); widen(2, 3, "s")
+        n_trans(0); x_trans(3, 0); stats(1); x_trans(2, 0); widen(3, 1, "v"); n_out(0); d_quant(0); root(1); x_out(3, 0, "s")
+        kr_passes(0); norm(1); kr_passes(1); widen(7, 2, "s"); x_quant(3); x_out(2, 0, "s"); n_trans(1); widen(3, 0, "v")
+        widen(4, 0, "s"); n_quant(0); lat_pass(3, 0); widen(3, 2, "v"); lat_pass(3, 1); n_out(1); widen(2, 1, "v")
+        lat_pass(3, 2); x_out(2, 1, "s"); widen(3, 3, "v"); kr_passes(3); n_quant(1); widen(7, 3, "s"); kv_mm(0, 0)
+        d_inter(2); kv_mm(1, 1); kv_out(0, 0, "s"); kv_mm(1, 0); kv_mm(0, 1); kv_out(1, 1, "s"); lat_pass(3, 3)
+        x_quant(2); stats(3); d_quant(2); lat_pass(2, 0); kv_out(0, 1, "s"); lat_pass(2, 1); d_inter(3); kr_passes(2)
+        root(3); kv_out(1, 0, "s"); kv_mm(1, 2); lat_pass(2, 2); widen(4, 3, "s"); lat_pass(2, 3); kv_mm(0, 2)
+        norm(3); kv_out(1, 2, "s"); d_quant(3); stats(2); n_trans(3); widen(7, 1, "v"); kv_out(0, 2, "s"); widen(4, 2, "v")
+        kv_mm(1, 3); widen(5, 1, "v"); kv_mm(0, 3); root(2); n_out(3); widen(6, 0, "v"); kv_out(1, 3, "s"); norm(2)
+        kv_out(0, 3, "s"); n_quant(3); widen(5, 0, "v"); widen(6, 1, "s"); n_trans(2); widen(4, 1, "v"); kv_mm(3, 0)
+        widen(5, 2, "v"); n_out(2); kv_mm(3, 1); d_inter(4); kv_out(3, 0, "s"); kv_mm(3, 3); kv_mm(3, 2); kv_out(3, 1, "s")
+        kv_out(3, 2, "s"); n_quant(2); widen(5, 3, "v"); kv_mm(2, 0); d_quant(4); kv_out(3, 3, "s"); kv_mm(2, 1)
+        kv_mm(2, 3); d_inter(5); kv_out(2, 0, "s"); kv_mm(2, 2); kv_mm(3, 4); kv_out(2, 1, "s"); kv_mm(0, 4); kv_mm(2, 4)
+        kv_out(2, 2, "s"); kv_mm(1, 4); widen(6, 3, "v"); d_quant(5); kv_out(2, 3, "s"); widen(6, 2, "v"); kv_out(1, 4, "s")
+        kv_mm(1, 5); widen(7, 0, "v"); kv_mm(3, 5); kv_out(2, 4, "s"); d_inter(6); kv_mm(2, 5); kv_mm(0, 5); kv_out(1, 5, "s")
+        kv_out(0, 5, "s"); d_inter(7); kv_out(2, 5, "s"); kv_out(3, 4, "s"); d_quant(6); kv_out(0, 4, "s"); d_quant(7)
+        kv_mm(3, 6); kv_out(3, 5, "v"); kv_mm(0, 6); kv_out(3, 6, "s"); rope(); kv_mm(3, 7); kv_mm(1, 7); kv_out(3, 7, "s")
+        kv_mm(2, 7); kv_mm(1, 6); kv_mm(2, 6); kv_mm(0, 7); kv_out(2, 6, "s"); kv_out(2, 7, "v"); kv_out(0, 7, "v")
+        kv_out(1, 7, "v"); kv_out(0, 6, "v"); kv_out(1, 6, "v")

@@ -21,19 +21,20 @@ NB = T // P
 NP = C // 512
 CHUNKS = [(512 * c, 512) for c in range(8)]
 NCH = len(CHUNKS)
-BLOADS = [(0, 512), (512, 512), (1024, 1024), (2048, 2048)]
-SPLIT = 320
+BLOADS = [(0, 512), (512, 1536), (2048, 2048)]
+WSPLIT = [352, 416, 64, 448]
+DSPLIT = [320, 448, 416, 480, 512, 416, 512, 512]
 
 
 def tile_multiheadlatentattention_pa_kernel(tc, x, freq_cis, Wckv, kv_norm_w, Wdkv_bytes, Wdkv_scale, out_0, out_1):
     nc = tc.nc
-    xf = x.flatten_outer_dims()
-    kvf = out_0.flatten_outer_dims()
-    krf = out_1.flatten_outer_dims()
+    xv = x.flatten_outer_dims().rearrange("(p b) c -> p b c", b=NB)
+    kvv = out_0.flatten_outer_dims().rearrange("(p b) n -> p b n", b=NB)
+    krv = out_1.flatten_outer_dims().rearrange("(p b) f -> p (b f)", b=NB)
 
     with ExitStack() as ctx:
         keep = ctx.enter_context(tc.tile_pool(name="keep", bufs=1))
-        work = ctx.enter_context(tc.tile_pool(name="work", bufs=3))
+        work = ctx.enter_context(tc.tile_pool(name="work", bufs=4))
         outs = ctx.enter_context(tc.tile_pool(name="outs", bufs=8))
         psum = ctx.enter_context(tc.psum_pool(name="psum", bufs=1))
         ctx.enter_context(tc.manual_schedule())
@@ -46,14 +47,17 @@ def tile_multiheadlatentattention_pa_kernel(tc, x, freq_cis, Wckv, kv_norm_w, Wd
         dummy = keep.tile([P, 1], F32, name="dummy")
         scale = keep.tile([P, 4], F32, name="scale")
         fr = keep.tile([P, NB * 64, 2], BF16, name="fr")
-        ss = keep.tile([P, NB * 64, 2], F32, name="ss")
+        nsin = keep.tile([P, NB * 64, 1], F32, name="nsin")
         xraw = [keep.tile([P, C], BF16, name="xraw%d" % b) for b in range(NB)]
         wraw = [keep.tile([P, 4, WIDTH], BF16, name="wraw%d" % g) for g in range(NP)]
         wb = [keep.tile([P, 4, n], U8, name="wb%d" % i) for i, (o, n) in enumerate(BLOADS)]
         xc = [keep.tile([P, NP, P], U32, name="xc%d" % b, align_bytes=64) for b in range(NB)]
         xs = [keep.tile([P, NP, P], U8, name="xs%d" % b, align_bytes=64) for b in range(NB)]
-        wc = [keep.tile([P, WIDTH], U32, name="wc%d" % g, align_bytes=64) for g in range(NP)]
-        ws = [keep.tile([P, WIDTH], U8, name="ws%d" % g, align_bytes=64) for g in range(NP)]
+        wc = [keep.tile([P, LORA], U32, name="wc%d" % g, align_bytes=64) for g in range(NP)]
+        ws = [keep.tile([P, LORA], U8, name="ws%d" % g, align_bytes=64) for g in range(NP)]
+        wrg = keep.tile([P, NP, ROPE, 4], BF16, name="wrg", align_bytes=64)
+        wrc = keep.tile([P, NP, ROPE], U32, name="wrc", align_bytes=64)
+        wrs = keep.tile([P, NP, ROPE], U8, name="wrs", align_bytes=64)
         ncod = [keep.tile([P, P], U32, name="ncod%d" % b, align_bytes=64) for b in range(NB)]
         nsc = [keep.tile([P, P], U8, name="nsc%d" % b, align_bytes=64) for b in range(NB)]
         dc = [keep.tile([P, CHUNKS[c][1]], U32, name="dc%d" % c, align_bytes=64) for c in range(NCH)]
@@ -65,41 +69,36 @@ def tile_multiheadlatentattention_pa_kernel(tc, x, freq_cis, Wckv, kv_norm_w, Wd
         bv = Wdkv_bytes.rearrange("(p j) n -> p j n", j=4)
 
         def load_x(b):
-            nc.sync.dma_start(out=xraw[b][:], in_=xf[b * P : (b + 1) * P, :])
+            nc.sync.dma_start(out=xraw[b][:], in_=xv[:, b, :])
 
         def load_w(g):
             nc.sync.dma_start(out=wraw[g][:], in_=wv[g])
 
-        nc.vector.memset(grow[:], 0.0)
+        nc.vector.memset(grow[:].bitcast(U32), 0)
         def load_b(c):
             o, n = BLOADS[c]
             nc.sync.dma_start(out=wb[c][:], in_=bv[:, :, o : o + n])
 
         nc.sync.dma_start(out=scale[:], in_=Wdkv_scale.rearrange("(p j) o -> p (j o)", j=4))
-        load_w(0)
-        load_x(0)
-        load_w(1)
-        load_w(2)
-        load_w(3)
         load_b(0)
         load_b(1)
+        load_x(0)
+        load_w(0)
+        load_w(1)
         nc.scalar.dma_start(out=grow[0:1, :], in_=kv_norm_w.rearrange("(o n) -> o n", o=1))
+        load_w(2)
+        load_w(3)
         load_x(1)
         load_x(2)
         load_x(3)
+        nc.sync.dma_start(out=fr[:].rearrange("p i e -> p (i e)"), in_=freq_cis.rearrange("(p b) i e -> p (b i e)", b=NB))
         load_b(2)
-        load_b(3)
-        nc.sync.dma_start(
-            out=fr[:].rearrange("p (b i) e -> p b (i e)", b=NB),
-            in_=freq_cis.rearrange("(b p) i e -> p b (i e)", p=P),
-        )
 
         make_identity(nc, ident[:])
         nc.vector.memset(ones[:], 1.0)
         nc.vector.memset(eps[:], 1e-6)
         nc.scalar.activation(dummy[:], eps[:], ACT.Abs_reciprocal_sqrt)
-        nc.gpsimd.tensor_scalar(ss[:, :, 0:1], fr[:, :, 1:2], 1.0, 0.0, ALU.mult, ALU.add)
-        nc.gpsimd.tensor_scalar(ss[:, :, 1:2], fr[:, :, 1:2], -1.0, 0.0, ALU.mult, ALU.add)
+        nc.gpsimd.tensor_scalar(nsin[:], fr[:, :, 1:2], -1.0, 0.0, ALU.mult, ALU.add)
 
         def four(t):
             return t.rearrange("p (c i) t -> p c t i", i=4)
@@ -115,8 +114,7 @@ def tile_multiheadlatentattention_pa_kernel(tc, x, freq_cis, Wckv, kv_norm_w, Wd
         lat = {}
         ng = {}
         nb = {}
-        kr = psum.tile([P, NB, P], F32, name="kr")
-        idle = list(range(7))
+        idle = list(range(8))
 
         def take():
             i = idle[0]
@@ -126,19 +124,27 @@ def tile_multiheadlatentattention_pa_kernel(tc, x, freq_cis, Wckv, kv_norm_w, Wd
 
         def wg_tile(g):
             if g not in wg:
-                wg[g] = work.tile([P, WIDTH, 4], BF16, name="wg", align_bytes=64)
+                wg[g] = work.tile([P, LORA, 4], BF16, name="wg", align_bytes=64)
             return wg[g]
 
         def w_inter_v(g):
-            nc.vector.tensor_copy(four(wg_tile(g)[:, 0:SPLIT, :]), by_four(wraw[g][:, :, 0:SPLIT]))
+            nc.vector.tensor_copy(four(wg_tile(g)[:, 0 : WSPLIT[g], :]), by_four(wraw[g][:, :, 0 : WSPLIT[g]]))
 
         def w_inter_s(g):
-            nc.scalar.copy(four(wg_tile(g)[:, SPLIT:WIDTH, :]), by_four(wraw[g][:, :, SPLIT:WIDTH]))
+            nc.scalar.copy(four(wg_tile(g)[:, WSPLIT[g] : LORA, :]), by_four(wraw[g][:, :, WSPLIT[g] : LORA]))
 
         def w_quant(g):
-            flat = wg[g][:].rearrange("p w j -> p (w j)")
-            nc.vector.quantize_mx(out=wc[g][:, 0:LORA].bitcast(FP8X4), scales=ws[g][:, 0:LORA], in_=flat[:, 0 : 4 * LORA])
-            nc.vector.quantize_mx(out=wc[g][:, LORA:WIDTH].bitcast(FP8X4), scales=ws[g][:, LORA:WIDTH], in_=flat[:, 4 * LORA : 4 * WIDTH])
+            nc.vector.quantize_mx(out=wc[g][:].bitcast(FP8X4), scales=ws[g][:], in_=wg[g][:].rearrange("p w j -> p (w j)"))
+
+        def wr_inter(g, eng):
+            copy(eng, four(wrg[:, g, :, :]), by_four(wraw[g][:, :, LORA:WIDTH]))
+
+        def wr_quant():
+            nc.vector.quantize_mx(
+                out=wrc[:].rearrange("p g w -> p (g w)").bitcast(FP8X4),
+                scales=wrs[:].rearrange("p g w -> p (g w)"),
+                in_=wrg[:].rearrange("p g w j -> p (g w j)"),
+            )
 
         def x_trans(b, h):
             words = xraw[b][:].bitcast(F32)
@@ -180,20 +186,23 @@ def tile_multiheadlatentattention_pa_kernel(tc, x, freq_cis, Wckv, kv_norm_w, Wd
                 out=lat[b][1][:],
                 lhsT=xc[b][:, g, :].bitcast(FP8X4),
                 lhsT_scale=xs[b][:, g, :],
-                rhs=wc[g][:, 0:LORA].bitcast(FP8X4),
-                rhs_scale=ws[g][:, 0:LORA],
+                rhs=wc[g][:].bitcast(FP8X4),
+                rhs_scale=ws[g][:],
                 start=(g == 0),
                 stop=(g == NP - 1),
             )
 
         def kr_passes(b):
+            if b % 2 == 0:
+                tp[("kr", b // 2)] = take()
+            kr = tp[("kr", b // 2)][1][:, 128 * (b % 2) : 128 * (b % 2 + 1)]
             for g in range(NP):
                 nc.tensor.matmul_mx(
-                    out=kr[:, b, :],
+                    out=kr,
                     lhsT=xc[b][:, g, :].bitcast(FP8X4),
                     lhsT_scale=xs[b][:, g, :],
-                    rhs=wc[g][:, LORA:WIDTH].bitcast(FP8X4),
-                    rhs_scale=ws[g][:, LORA:WIDTH],
+                    rhs=wrc[:, g, :].bitcast(FP8X4),
+                    rhs_scale=wrs[:, g, :],
                     start=(g == 0),
                     stop=(g == NP - 1),
                 )
@@ -216,10 +225,11 @@ def tile_multiheadlatentattention_pa_kernel(tc, x, freq_cis, Wckv, kv_norm_w, Wd
             for u in range(2):
                 nc.tensor.transpose(tp[(b, 2)][1][:, P * u : P * (u + 1)], words[:, u::2], ident[:])
 
-        def n_out(b):
+        def n_out(b, eng):
             ng[b] = work.tile([P, P, 4], BF16, name="ng", align_bytes=64)
             i, t = tp[(b, 2)]
-            nc.scalar.copy(
+            copy(
+                eng,
                 ng[b][:].rearrange("p r t -> p (r t)").bitcast(F32).rearrange("p (r u) -> p r u", u=2),
                 t[:, 0 : 2 * P].rearrange("p (u r) -> p r u", u=2),
             )
@@ -237,7 +247,7 @@ def tile_multiheadlatentattention_pa_kernel(tc, x, freq_cis, Wckv, kv_norm_w, Wd
         def widen(c, j, eng):
             t, o, n = bytes_of(c)
             if c not in wide:
-                wide[c] = keep.tile([P, 4, n], BF16, name="wide%d" % c)
+                wide[c] = work.tile([P, 4, n], BF16, name="wide", bufs=5)
             w = wide[c][:, j, :]
             b = t[:, j, o : o + n].bitcast(FP8)
             if eng == "v":
@@ -245,9 +255,17 @@ def tile_multiheadlatentattention_pa_kernel(tc, x, freq_cis, Wckv, kv_norm_w, Wd
             else:
                 nc.scalar.activation(w, b, ACT.Copy, scale=scale[:, j : j + 1])
 
-        def d_inter(c):
-            dg[c] = work.tile([P, CHUNKS[c][1], 4], BF16, name="dg", align_bytes=64)
-            nc.vector.tensor_copy(four(dg[c][:]), by_four(wide[c][:]))
+        def dg_tile(c):
+            if c not in dg:
+                dg[c] = work.tile([P, CHUNKS[c][1], 4], BF16, name="dg", align_bytes=64)
+            return dg[c]
+
+        def d_inter_v(c):
+            nc.vector.tensor_copy(four(dg_tile(c)[:, 0 : DSPLIT[c], :]), by_four(wide[c][:, :, 0 : DSPLIT[c]]))
+
+        def d_inter_s(c):
+            n = CHUNKS[c][1]
+            nc.scalar.copy(four(dg_tile(c)[:, DSPLIT[c] : n, :]), by_four(wide[c][:, :, DSPLIT[c] : n]))
 
         def d_quant(c):
             nc.vector.quantize_mx(out=dc[c][:].bitcast(FP8X4), scales=ds[c][:], in_=dg[c][:].rearrange("p w j -> p (w j)"))
@@ -275,53 +293,61 @@ def tile_multiheadlatentattention_pa_kernel(tc, x, freq_cis, Wckv, kv_norm_w, Wd
             idle.append(i)
             if not first:
                 m = c // 2
-                nc.sync.dma_start(out=kvf[b * P : (b + 1) * P, 1024 * m : 1024 * (m + 1)], in_=tp[key][:])
+                nc.sync.dma_start(out=kvv[:, b, 1024 * m : 1024 * (m + 1)], in_=tp[key][:])
 
-        def rope():
-            k2 = kr[:].rearrange("p b (i e) -> p (b i) e", e=2)
-            t1 = work.tile([P, NB * 64, 2], F32, name="t1", bufs=1)
-            t2 = work.tile([P, NB * 64, 2], F32, name="t2", bufs=1)
-            ro = work.tile([P, NB * 64, 2], F32, name="ro", bufs=1)
-            nc.vector.tensor_tensor(t1[:], k2, fr[:, :, 0:1].to_broadcast([P, NB * 64, 2]), ALU.mult)
-            nc.vector.tensor_tensor(t2[:], k2, ss[:], ALU.mult)
-            nc.vector.tensor_tensor(ro[:], t1[:], t2[:, :, ::-1], ALU.add)
-            nc.sync.dma_start(
-                out=krf.rearrange("(b p) f -> p b f", p=P),
-                in_=ro[:].rearrange("p (b i) e -> p b (i e)", b=NB),
-            )
+        def rope(h):
+            pairs = slice(128 * h, 128 * (h + 1))
+            cos, sin = fr[:, pairs, 0:1], fr[:, pairs, 1:2]
+            i, t = tp[("kr", h)]
+            k2 = t[:, 0:256].rearrange("p (i e) -> p i e", e=2)
+            t1 = work.tile([P, 128, 2], F32, name="t1", bufs=2)
+            t2 = work.tile([P, 2, 128], F32, name="t2", bufs=2)
+            ro = work.tile([P, 128, 2], F32, name="ro", bufs=2)
+            nc.vector.tensor_tensor(t1[:], k2, cos.to_broadcast([P, 128, 2]), ALU.mult)
+            nc.vector.tensor_tensor(t2[:, 0, :].unsqueeze(2), k2[:, :, 1:2], nsin[:, pairs, :], ALU.mult)
+            nc.vector.tensor_tensor(t2[:, 1, :].unsqueeze(2), k2[:, :, 0:1], sin, ALU.mult)
+            idle.append(i)
+            nc.vector.tensor_tensor(ro[:], t1[:], t2[:].rearrange("p e i -> p i e"), ALU.add)
+            nc.sync.dma_start(out=krv[:, 256 * h : 256 * (h + 1)], in_=ro[:].rearrange("p i e -> p (i e)"))
 
         def gains():
             tp["gain"] = take()
             nc.tensor.matmul(tp["gain"][1][:], lhsT=ones[:], rhs=grow[:], start=True, stop=True)
 
-        def gain_out():
+        def gain_out(eng):
             i, t = tp["gain"]
-            nc.scalar.copy(gain[:], t[:])
+            copy(eng, gain[:], t[:])
             idle.append(i)
 
-        w_inter_v(0); w_inter_s(0); x_trans(0, 0); w_quant(0); x_trans(0, 1); x_out(0, 0, "s"); w_inter_v(1); w_inter_s(1)
-        x_out(0, 1, "v"); w_inter_v(2); w_inter_s(2); x_quant(0); w_quant(1); lat_pass(0, 0); w_inter_s(3); w_inter_v(3)
-        lat_pass(0, 1); w_quant(2); gains(); widen(0, 0, "s"); widen(1, 0, "v"); lat_pass(0, 2); widen(1, 2, "v")
-        gain_out(); widen(1, 1, "v"); x_trans(1, 1); w_quant(3); widen(1, 3, "s"); x_trans(1, 0); x_out(1, 1, "s")
-        widen(0, 3, "v"); x_trans(2, 1); d_inter(1); x_out(1, 0, "s"); lat_pass(0, 3); widen(0, 2, "s"); x_trans(3, 1)
-        stats(0); x_quant(1); widen(0, 1, "s"); d_quant(1); lat_pass(1, 0); root(0); widen(2, 0, "v"); x_out(3, 1, "s")
-        norm(0); lat_pass(1, 1); widen(2, 2, "s"); lat_pass(1, 2); d_inter(0); lat_pass(1, 3); widen(2, 3, "s")
-        n_trans(0); x_trans(3, 0); stats(1); x_trans(2, 0); widen(3, 1, "v"); n_out(0); d_quant(0); root(1); x_out(3, 0, "s")
-        kr_passes(0); norm(1); kr_passes(1); widen(7, 2, "s"); x_quant(3); x_out(2, 0, "s"); n_trans(1); widen(3, 0, "v")
-        widen(4, 0, "s"); n_quant(0); lat_pass(3, 0); widen(3, 2, "v"); lat_pass(3, 1); n_out(1); widen(2, 1, "v")
-        lat_pass(3, 2); x_out(2, 1, "s"); widen(3, 3, "v"); kr_passes(3); n_quant(1); widen(7, 3, "s"); kv_mm(0, 0)
-        d_inter(2); kv_mm(1, 1); kv_out(0, 0, "s"); kv_mm(1, 0); kv_mm(0, 1); kv_out(1, 1, "s"); lat_pass(3, 3)
-        x_quant(2); stats(3); d_quant(2); lat_pass(2, 0); kv_out(0, 1, "s"); lat_pass(2, 1); d_inter(3); kr_passes(2)
-        root(3); kv_out(1, 0, "s"); kv_mm(1, 2); lat_pass(2, 2); widen(4, 3, "s"); lat_pass(2, 3); kv_mm(0, 2)
-        norm(3); kv_out(1, 2, "s"); d_quant(3); stats(2); n_trans(3); widen(7, 1, "v"); kv_out(0, 2, "s"); widen(4, 2, "v")
-        kv_mm(1, 3); widen(5, 1, "v"); kv_mm(0, 3); root(2); n_out(3); widen(6, 0, "v"); kv_out(1, 3, "s"); norm(2)
-        kv_out(0, 3, "s"); n_quant(3); widen(5, 0, "v"); widen(6, 1, "s"); n_trans(2); widen(4, 1, "v"); kv_mm(3, 0)
-        widen(5, 2, "v"); n_out(2); kv_mm(3, 1); d_inter(4); kv_out(3, 0, "s"); kv_mm(3, 3); kv_mm(3, 2); kv_out(3, 1, "s")
-        kv_out(3, 2, "s"); n_quant(2); widen(5, 3, "v"); kv_mm(2, 0); d_quant(4); kv_out(3, 3, "s"); kv_mm(2, 1)
-        kv_mm(2, 3); d_inter(5); kv_out(2, 0, "s"); kv_mm(2, 2); kv_mm(3, 4); kv_out(2, 1, "s"); kv_mm(0, 4); kv_mm(2, 4)
-        kv_out(2, 2, "s"); kv_mm(1, 4); widen(6, 3, "v"); d_quant(5); kv_out(2, 3, "s"); widen(6, 2, "v"); kv_out(1, 4, "s")
-        kv_mm(1, 5); widen(7, 0, "v"); kv_mm(3, 5); kv_out(2, 4, "s"); d_inter(6); kv_mm(2, 5); kv_mm(0, 5); kv_out(1, 5, "s")
-        kv_out(0, 5, "s"); d_inter(7); kv_out(2, 5, "s"); kv_out(3, 4, "s"); d_quant(6); kv_out(0, 4, "s"); d_quant(7)
-        kv_mm(3, 6); kv_out(3, 5, "v"); kv_mm(0, 6); kv_out(3, 6, "s"); rope(); kv_mm(3, 7); kv_mm(1, 7); kv_out(3, 7, "s")
-        kv_mm(2, 7); kv_mm(1, 6); kv_mm(2, 6); kv_mm(0, 7); kv_out(2, 6, "s"); kv_out(2, 7, "v"); kv_out(0, 7, "v")
-        kv_out(1, 7, "v"); kv_out(0, 6, "v"); kv_out(1, 6, "v")
+        gains(); widen(0, 2, "s"); widen(0, 3, "v"); widen(0, 1, "v"); widen(0, 0, "v"); d_inter_s(0)
+        d_inter_v(0); widen(1, 2, "v"); widen(1, 0, "v"); widen(2, 0, "v"); widen(1, 1, "v"); d_quant(0)
+        widen(1, 3, "s"); d_inter_v(1); widen(3, 3, "s"); widen(3, 0, "s"); w_inter_v(0); widen(2, 3, "v")
+        w_inter_v(1); d_inter_s(1); widen(2, 2, "s"); x_trans(0, 0); x_out(0, 0, "s"); w_inter_s(0)
+        x_trans(0, 1); x_out(0, 1, "s"); x_quant(0); w_inter_v(2); w_quant(0); lat_pass(0, 0); widen(2, 1, "s")
+        w_inter_s(1); w_quant(1); lat_pass(0, 1); w_inter_v(3); w_inter_s(2); w_quant(2); widen(3, 2, "s")
+        w_inter_s(3); w_quant(3); widen(3, 1, "s"); d_inter_v(2); x_trans(1, 0); x_out(1, 0, "s"); x_trans(1, 1)
+        x_out(1, 1, "s"); x_quant(1); d_inter_v(3); lat_pass(0, 2); lat_pass(0, 3); stats(0); gain_out("s")
+        x_trans(2, 0); x_trans(2, 1); x_out(2, 1, "s"); x_trans(3, 1); root(0); norm(0); x_out(2, 0, "s")
+        x_quant(2); lat_pass(1, 0); lat_pass(1, 1); lat_pass(1, 2); d_inter_s(2); x_out(3, 1, "s"); d_quant(1)
+        d_quant(2); x_trans(3, 0); x_out(3, 0, "s"); n_trans(0); n_out(0, "s"); lat_pass(1, 3); stats(1)
+        d_inter_s(3); root(1); lat_pass(2, 0); lat_pass(2, 1); lat_pass(2, 2); lat_pass(2, 3); stats(2)
+        n_quant(0); kv_mm(0, 1); kv_out(0, 1, "s"); kv_mm(0, 0); kv_out(0, 0, "s"); root(2); x_quant(3)
+        lat_pass(3, 0); lat_pass(3, 1); lat_pass(3, 2); lat_pass(3, 3); stats(3); widen(6, 2, "v"); norm(1)
+        n_trans(1); n_out(1, "s"); kv_mm(0, 2); kv_out(0, 2, "s"); root(3); widen(7, 2, "v"); d_quant(3)
+        kv_mm(0, 3); kv_out(0, 3, "s"); widen(6, 3, "v"); norm(2); n_trans(2); widen(4, 1, "v"); n_quant(1)
+        widen(7, 3, "v"); widen(6, 1, "v"); norm(3); widen(7, 0, "v"); n_out(2, "s"); n_quant(2)
+        widen(7, 1, "v"); widen(6, 0, "v"); kv_mm(1, 3); kv_out(1, 3, "s"); kv_mm(1, 1); kv_mm(1, 2)
+        kv_out(1, 2, "s"); n_trans(3); n_out(3, "v"); widen(4, 3, "v"); kv_out(1, 1, "s"); kv_mm(1, 0)
+        kv_out(1, 0, "s"); kv_mm(2, 0); kv_mm(2, 1); kv_out(2, 0, "s"); kv_mm(2, 2); kv_out(2, 1, "s")
+        n_quant(3); kv_mm(3, 1); kv_mm(2, 3); kv_out(2, 3, "s"); kv_out(2, 2, "s"); d_inter_v(7)
+        widen(5, 2, "v"); kv_mm(3, 0); kv_mm(3, 2); kv_out(3, 0, "s"); kv_out(3, 1, "s"); kv_mm(3, 3)
+        kv_out(3, 3, "s"); d_quant(7); kv_mm(2, 7); kv_mm(0, 7); kv_out(3, 2, "s"); kv_mm(3, 7)
+        kv_out(3, 7, "s"); d_inter_v(6); widen(5, 0, "v"); d_quant(6); widen(4, 2, "v"); kv_mm(3, 6)
+        kv_out(3, 6, "s"); widen(4, 0, "v"); kv_out(2, 7, "s"); kv_mm(1, 6); kv_mm(2, 6); kv_out(2, 6, "s")
+        kv_mm(0, 6); kv_out(0, 6, "s"); kv_out(0, 7, "s"); widen(5, 3, "v"); d_inter_v(4); widen(5, 1, "v")
+        d_inter_s(5); kv_out(1, 6, "s"); kv_mm(1, 7); kv_out(1, 7, "s"); d_quant(4); kv_mm(1, 4); kv_mm(2, 4)
+        kv_out(1, 4, "s"); kv_mm(3, 4); d_inter_v(5); d_quant(5); kv_mm(1, 5); kv_out(1, 5, "s")
+        wr_inter(0, "v"); wr_inter(1, "v"); wr_inter(2, "v"); wr_inter(3, "v"); kv_out(3, 4, "v"); wr_quant()
+        kv_mm(0, 5); kv_out(0, 5, "v"); kv_out(2, 4, "v"); kv_mm(3, 5); kv_mm(2, 5); kv_out(3, 5, "s")
+        kv_mm(0, 4); kv_out(0, 4, "s"); kr_passes(0); kr_passes(1); rope(0); kv_out(2, 5, "s"); kr_passes(2)
+        kr_passes(3); rope(1)

from contextlib import ExitStack

import concourse.mybir as mybir
from concourse.masks import make_identity

T, C, LORA, ROPE, KVW = 512, 2048, 512, 128, 4096
WIDTH = LORA + ROPE
FLOPS = 2 * T * C * WIDTH + 2 * T * LORA * KVW

F32 = mybir.dt.float32
BF16 = mybir.dt.bfloat16
U32 = mybir.dt.uint32
U8 = mybir.dt.uint8
FP8 = mybir.dt.float8_e4m3fn
FP8X4 = mybir.dt.float8_e4m3fn_x4
ALU = mybir.AluOpType
ACT = mybir.ActivationFunctionType

P = 128
NB = T // P
NP = C // 512
CHUNKS = [(512 * c, 512) for c in range(8)]
NCH = len(CHUNKS)
BLOADS = [(0, 512), (512, 1536), (2048, 2048)]
WSPLIT = [352, 416, 64, 448]
DSPLIT = [320, 448, 416, 480, 512, 416, 512, 512]


def tile_multiheadlatentattention_pa_kernel(tc, x, freq_cis, Wckv, kv_norm_w, Wdkv_bytes, Wdkv_scale, out_0, out_1):
    nc = tc.nc
    xv = x.flatten_outer_dims().rearrange("(p b) c -> p b c", b=NB)
    kvv = out_0.flatten_outer_dims().rearrange("(p b) n -> p b n", b=NB)
    krv = out_1.flatten_outer_dims().rearrange("(p b) f -> p (b f)", b=NB)

    with ExitStack() as ctx:
        keep = ctx.enter_context(tc.tile_pool(name="keep", bufs=1))
        work = ctx.enter_context(tc.tile_pool(name="work", bufs=4))
        outs = ctx.enter_context(tc.tile_pool(name="outs", bufs=8))
        psum = ctx.enter_context(tc.psum_pool(name="psum", bufs=1))
        ctx.enter_context(tc.manual_schedule())

        ident = keep.tile([P, P], F32, name="ident")
        ones = keep.tile([P, P], BF16, name="ones")
        grow = keep.tile([P, LORA], BF16, name="grow")
        gain = keep.tile([P, LORA], F32, name="gain")
        eps = keep.tile([P, 1], F32, name="eps")
        dummy = keep.tile([P, 1], F32, name="dummy")
        scale = keep.tile([P, 4], F32, name="scale")
        fr = keep.tile([P, NB * 64, 2], BF16, name="fr")
        nsin = keep.tile([P, NB * 64, 1], F32, name="nsin")
        xraw = [keep.tile([P, C], BF16, name="xraw%d" % b) for b in range(NB)]
        wraw = [keep.tile([P, 4, WIDTH], BF16, name="wraw%d" % g) for g in range(NP)]
        wb = [keep.tile([P, 4, n], U8, name="wb%d" % i) for i, (o, n) in enumerate(BLOADS)]
        xc = [keep.tile([P, NP, P], U32, name="xc%d" % b, align_bytes=64) for b in range(NB)]
        xs = [keep.tile([P, NP, P], U8, name="xs%d" % b, align_bytes=64) for b in range(NB)]
        wc = [keep.tile([P, LORA], U32, name="wc%d" % g, align_bytes=64) for g in range(NP)]
        ws = [keep.tile([P, LORA], U8, name="ws%d" % g, align_bytes=64) for g in range(NP)]
        wrg = keep.tile([P, NP, ROPE, 4], BF16, name="wrg", align_bytes=64)
        wrc = keep.tile([P, NP, ROPE], U32, name="wrc", align_bytes=64)
        wrs = keep.tile([P, NP, ROPE], U8, name="wrs", align_bytes=64)
        ncod = [keep.tile([P, P], U32, name="ncod%d" % b, align_bytes=64) for b in range(NB)]
        nsc = [keep.tile([P, P], U8, name="nsc%d" % b, align_bytes=64) for b in range(NB)]
        dc = [keep.tile([P, CHUNKS[c][1]], U32, name="dc%d" % c, align_bytes=64) for c in range(NCH)]
        ds = [keep.tile([P, CHUNKS[c][1]], U8, name="ds%d" % c, align_bytes=64) for c in range(NCH)]
        sumsq = [keep.tile([P, 1], F32, name="sumsq%d" % b) for b in range(NB)]
        rstd = [keep.tile([P, 1], F32, name="rstd%d" % b) for b in range(NB)]

        wv = Wckv.rearrange("(g p j) n -> g p j n", p=P, j=4)
        bv = Wdkv_bytes.rearrange("(p j) n -> p j n", j=4)

        def load_x(b):
            nc.sync.dma_start(out=xraw[b][:], in_=xv[:, b, :])

        def load_w(g):
            nc.sync.dma_start(out=wraw[g][:], in_=wv[g])

        nc.vector.memset(grow[:].bitcast(U32), 0)
        def load_b(c):
            o, n = BLOADS[c]
            nc.sync.dma_start(out=wb[c][:], in_=bv[:, :, o : o + n])

        nc.sync.dma_start(out=scale[:], in_=Wdkv_scale.rearrange("(p j) o -> p (j o)", j=4))
        load_b(0)
        load_b(1)
        load_x(0)
        load_w(0)
        load_w(1)
        nc.scalar.dma_start(out=grow[0:1, :], in_=kv_norm_w.rearrange("(o n) -> o n", o=1))
        load_w(2)
        load_w(3)
        load_x(1)
        load_x(2)
        load_x(3)
        nc.sync.dma_start(out=fr[:].rearrange("p i e -> p (i e)"), in_=freq_cis.rearrange("(p b) i e -> p (b i e)", b=NB))
        load_b(2)

        make_identity(nc, ident[:])
        nc.vector.memset(ones[:], 1.0)
        nc.vector.memset(eps[:], 1e-6)
        nc.scalar.activation(dummy[:], eps[:], ACT.Abs_reciprocal_sqrt)
        nc.gpsimd.tensor_scalar(nsin[:], fr[:, :, 1:2], -1.0, 0.0, ALU.mult, ALU.add)

        def four(t):
            return t.rearrange("p (c i) t -> p c t i", i=4)

        def by_four(t):
            return t.rearrange("p t (c i) -> p c t i", i=4)

        wg = {}
        xg = {}
        wide = {}
        dg = {}
        tp = {}
        lat = {}
        ng = {}
        nb = {}
        idle = list(range(8))

        def take():
            i = idle[0]
            idle.remove(i)
            return i, psum.tile([P, 512], F32, name="bank%d" % i)


        def wg_tile(g):
            if g not in wg:
                wg[g] = work.tile([P, LORA, 4], BF16, name="wg", align_bytes=64)
            return wg[g]

        def w_inter_v(g):
            nc.vector.tensor_copy(four(wg_tile(g)[:, 0 : WSPLIT[g], :]), by_four(wraw[g][:, :, 0 : WSPLIT[g]]))

        def w_inter_s(g):
            nc.scalar.copy(four(wg_tile(g)[:, WSPLIT[g] : LORA, :]), by_four(wraw[g][:, :, WSPLIT[g] : LORA]))

        def w_quant(g):
            nc.vector.quantize_mx(out=wc[g][:].bitcast(FP8X4), scales=ws[g][:], in_=wg[g][:].rearrange("p w j -> p (w j)"))

        def wr_inter(g, eng):
            copy(eng, four(wrg[:, g, :, :]), by_four(wraw[g][:, :, LORA:WIDTH]))

        def wr_quant():
            nc.vector.quantize_mx(
                out=wrc[:].rearrange("p g w -> p (g w)").bitcast(FP8X4),
                scales=wrs[:].rearrange("p g w -> p (g w)"),
                in_=wrg[:].rearrange("p g w j -> p (g w j)"),
            )

        def x_trans(b, h):
            words = xraw[b][:].bitcast(F32)
            tp[(b, h)] = take()
            t = tp[(b, h)][1][:].rearrange("p (a r) -> p a r", a=4)
            for gg in range(2):
                for u in range(2):
                    nc.tensor.transpose(t[:, 2 * gg + u, :], words[:, 256 * (2 * h + gg) + u : 256 * (2 * h + gg + 1) : 2], ident[:])

        def copy(eng, out, in_):
            if eng == "v":
                nc.vector.tensor_copy(out, in_)
            else:
                nc.scalar.copy(out, in_)

        def x_out(b, h, eng):
            if b not in xg:
                xg[b] = work.tile([P, NP, P, 4], BF16, name="xg", align_bytes=64)
            flat = xg[b][:].rearrange("p g r t -> p (g r t)").bitcast(F32)
            i, t = tp[(b, h)]
            copy(
                eng,
                flat[:, 512 * h : 512 * (h + 1)].rearrange("p (g r u) -> p g r u", g=2, u=2),
                t[:].rearrange("p (g u r) -> p g r u", g=2, u=2),
            )
            idle.append(i)

        def x_quant(b):
            nc.vector.quantize_mx(
                out=xc[b][:].rearrange("p g r -> p (g r)").bitcast(FP8X4),
                scales=xs[b][:].rearrange("p g r -> p (g r)"),
                in_=xg[b][:].rearrange("p g r t -> p (g r t)"),
            )

        def lat_pass(b, g):
            if g == 0:
                lat[b] = take()
            nc.tensor.matmul_mx(
                out=lat[b][1][:],
                lhsT=xc[b][:, g, :].bitcast(FP8X4),
                lhsT_scale=xs[b][:, g, :],
                rhs=wc[g][:].bitcast(FP8X4),
                rhs_scale=ws[g][:],
                start=(g == 0),
                stop=(g == NP - 1),
            )

        def kr_passes(b):
            if b % 2 == 0:
                tp[("kr", b // 2)] = take()
            kr = tp[("kr", b // 2)][1][:, 128 * (b % 2) : 128 * (b % 2 + 1)]
            for g in range(NP):
                nc.tensor.matmul_mx(
                    out=kr,
                    lhsT=xc[b][:, g, :].bitcast(FP8X4),
                    lhsT_scale=xs[b][:, g, :],
                    rhs=wrc[:, g, :].bitcast(FP8X4),
                    rhs_scale=wrs[:, g, :],
                    start=(g == 0),
                    stop=(g == NP - 1),
                )

        def stats(b):
            sq = work.tile([P, LORA], BF16, name="sq")
            nc.scalar.activation(sq[:], lat[b][1][:], ACT.Square, accum_out=sumsq[b][:])

        def root(b):
            nc.scalar.activation(rstd[b][:], sumsq[b][:], ACT.Abs_reciprocal_sqrt, bias=eps[:], scale=1.0 / LORA)

        def norm(b):
            nb[b] = work.tile([P, LORA], BF16, name="nb")
            nc.vector.scalar_tensor_tensor(nb[b][:], lat[b][1][:], rstd[b][:], gain[:], ALU.mult, ALU.mult)
            idle.append(lat[b][0])

        def n_trans(b):
            tp[(b, 2)] = take()
            words = nb[b][:].bitcast(F32)
            for u in range(2):
                nc.tensor.transpose(tp[(b, 2)][1][:, P * u : P * (u + 1)], words[:, u::2], ident[:])

        def n_out(b, eng):
            ng[b] = work.tile([P, P, 4], BF16, name="ng", align_bytes=64)
            i, t = tp[(b, 2)]
            copy(
                eng,
                ng[b][:].rearrange("p r t -> p (r t)").bitcast(F32).rearrange("p (r u) -> p r u", u=2),
                t[:, 0 : 2 * P].rearrange("p (u r) -> p r u", u=2),
            )
            idle.append(i)

        def n_quant(b):
            nc.vector.quantize_mx(out=ncod[b][:].bitcast(FP8X4), scales=nsc[b][:], in_=ng[b][:].rearrange("p r t -> p (r t)"))

        def bytes_of(c):
            o, n = CHUNKS[c]
            for i, (bo, bn) in enumerate(BLOADS):
                if bo <= o < bo + bn:
                    return wb[i], o - bo, n

        def widen(c, j, eng):
            t, o, n = bytes_of(c)
            if c not in wide:
                wide[c] = work.tile([P, 4, n], BF16, name="wide", bufs=5)
            w = wide[c][:, j, :]
            b = t[:, j, o : o + n].bitcast(FP8)
            if eng == "v":
                nc.vector.tensor_scalar(w, b, scale[:, j : j + 1], None, ALU.mult)
            else:
                nc.scalar.activation(w, b, ACT.Copy, scale=scale[:, j : j + 1])

        def dg_tile(c):
            if c not in dg:
                dg[c] = work.tile([P, CHUNKS[c][1], 4], BF16, name="dg", align_bytes=64)
            return dg[c]

        def d_inter_v(c):
            nc.vector.tensor_copy(four(dg_tile(c)[:, 0 : DSPLIT[c], :]), by_four(wide[c][:, :, 0 : DSPLIT[c]]))

        def d_inter_s(c):
            n = CHUNKS[c][1]
            nc.scalar.copy(four(dg_tile(c)[:, DSPLIT[c] : n, :]), by_four(wide[c][:, :, DSPLIT[c] : n]))

        def d_quant(c):
            nc.vector.quantize_mx(out=dc[c][:].bitcast(FP8X4), scales=ds[c][:], in_=dg[c][:].rearrange("p w j -> p (w j)"))

        def kv_mm(b, c):
            n = CHUNKS[c][1]
            tp[("kv", b, c)] = take()
            nc.tensor.matmul_mx(
                out=tp[("kv", b, c)][1][:, 0:n],
                lhsT=ncod[b][:].bitcast(FP8X4),
                lhsT_scale=nsc[b][:],
                rhs=dc[c][:].bitcast(FP8X4),
                rhs_scale=ds[c][:],
                start=True,
                stop=True,
            )

        def kv_out(b, c, eng):
            i, t = tp[("kv", b, c)]
            key = ("o", b, c // 2)
            first = key not in tp
            if first:
                tp[key] = outs.tile([P, 1024], F32, name="o")
            copy(eng, tp[key][:, 512 * (c % 2) : 512 * (c % 2 + 1)], t[:])
            idle.append(i)
            if not first:
                m = c // 2
                nc.sync.dma_start(out=kvv[:, b, 1024 * m : 1024 * (m + 1)], in_=tp[key][:])

        def rope(h):
            pairs = slice(128 * h, 128 * (h + 1))
            cos, sin = fr[:, pairs, 0:1], fr[:, pairs, 1:2]
            i, t = tp[("kr", h)]
            k2 = t[:, 0:256].rearrange("p (i e) -> p i e", e=2)
            t1 = work.tile([P, 128, 2], F32, name="t1", bufs=2)
            t2 = work.tile([P, 2, 128], F32, name="t2", bufs=2)
            ro = work.tile([P, 128, 2], F32, name="ro", bufs=2)
            nc.vector.tensor_tensor(t1[:], k2, cos.to_broadcast([P, 128, 2]), ALU.mult)
            nc.vector.tensor_tensor(t2[:, 0, :].unsqueeze(2), k2[:, :, 1:2], nsin[:, pairs, :], ALU.mult)
            nc.vector.tensor_tensor(t2[:, 1, :].unsqueeze(2), k2[:, :, 0:1], sin, ALU.mult)
            idle.append(i)
            nc.vector.tensor_tensor(ro[:], t1[:], t2[:].rearrange("p e i -> p i e"), ALU.add)
            nc.sync.dma_start(out=krv[:, 256 * h : 256 * (h + 1)], in_=ro[:].rearrange("p i e -> p (i e)"))

        def gains():
            tp["gain"] = take()
            nc.tensor.matmul(tp["gain"][1][:], lhsT=ones[:], rhs=grow[:], start=True, stop=True)

        def gain_out(eng):
            i, t = tp["gain"]
            copy(eng, gain[:], t[:])
            idle.append(i)

        gains(); widen(0, 2, "s"); widen(0, 3, "v"); widen(0, 1, "v"); widen(0, 0, "v"); d_inter_s(0)
        d_inter_v(0); widen(1, 2, "v"); widen(1, 0, "v"); widen(2, 0, "v"); widen(1, 1, "v"); d_quant(0)
        widen(1, 3, "s"); d_inter_v(1); widen(3, 3, "s"); widen(3, 0, "s"); w_inter_v(0); widen(2, 3, "v")
        w_inter_v(1); d_inter_s(1); widen(2, 2, "s"); x_trans(0, 0); x_out(0, 0, "s"); w_inter_s(0)
        x_trans(0, 1); x_out(0, 1, "s"); x_quant(0); w_inter_v(2); w_quant(0); lat_pass(0, 0); widen(2, 1, "s")
        w_inter_s(1); w_quant(1); lat_pass(0, 1); w_inter_v(3); w_inter_s(2); w_quant(2); widen(3, 2, "s")
        w_inter_s(3); w_quant(3); widen(3, 1, "s"); d_inter_v(2); x_trans(1, 0); x_out(1, 0, "s"); x_trans(1, 1)
        x_out(1, 1, "s"); x_quant(1); d_inter_v(3); lat_pass(0, 2); lat_pass(0, 3); stats(0); gain_out("s")
        x_trans(2, 0); x_trans(2, 1); x_out(2, 1, "s"); x_trans(3, 1); root(0); norm(0); x_out(2, 0, "s")
        x_quant(2); lat_pass(1, 0); lat_pass(1, 1); lat_pass(1, 2); d_inter_s(2); x_out(3, 1, "s"); d_quant(1)
        d_quant(2); x_trans(3, 0); x_out(3, 0, "s"); n_trans(0); n_out(0, "s"); lat_pass(1, 3); stats(1)
        d_inter_s(3); root(1); lat_pass(2, 0); lat_pass(2, 1); lat_pass(2, 2); lat_pass(2, 3); stats(2)
        n_quant(0); kv_mm(0, 1); kv_out(0, 1, "s"); kv_mm(0, 0); kv_out(0, 0, "s"); root(2); x_quant(3)
        lat_pass(3, 0); lat_pass(3, 1); lat_pass(3, 2); lat_pass(3, 3); stats(3); widen(6, 2, "v"); norm(1)
        n_trans(1); n_out(1, "s"); kv_mm(0, 2); kv_out(0, 2, "s"); root(3); widen(7, 2, "v"); d_quant(3)
        kv_mm(0, 3); kv_out(0, 3, "s"); widen(6, 3, "v"); norm(2); n_trans(2); widen(4, 1, "v"); n_quant(1)
        widen(7, 3, "v"); widen(6, 1, "v"); norm(3); widen(7, 0, "v"); n_out(2, "s"); n_quant(2)
        widen(7, 1, "v"); widen(6, 0, "v"); kv_mm(1, 3); kv_out(1, 3, "s"); kv_mm(1, 1); kv_mm(1, 2)
        kv_out(1, 2, "s"); n_trans(3); n_out(3, "v"); widen(4, 3, "v"); kv_out(1, 1, "s"); kv_mm(1, 0)
        kv_out(1, 0, "s"); kv_mm(2, 0); kv_mm(2, 1); kv_out(2, 0, "s"); kv_mm(2, 2); kv_out(2, 1, "s")
        n_quant(3); kv_mm(3, 1); kv_mm(2, 3); kv_out(2, 3, "s"); kv_out(2, 2, "s"); d_inter_v(7)
        widen(5, 2, "v"); kv_mm(3, 0); kv_mm(3, 2); kv_out(3, 0, "s"); kv_out(3, 1, "s"); kv_mm(3, 3)
        kv_out(3, 3, "s"); d_quant(7); kv_mm(2, 7); kv_mm(0, 7); kv_out(3, 2, "s"); kv_mm(3, 7)
        kv_out(3, 7, "s"); d_inter_v(6); widen(5, 0, "v"); d_quant(6); widen(4, 2, "v"); kv_mm(3, 6)
        kv_out(3, 6, "s"); widen(4, 0, "v"); kv_out(2, 7, "s"); kv_mm(1, 6); kv_mm(2, 6); kv_out(2, 6, "s")
        kv_mm(0, 6); kv_out(0, 6, "s"); kv_out(0, 7, "s"); widen(5, 3, "v"); d_inter_v(4); widen(5, 1, "v")
        d_inter_s(5); kv_out(1, 6, "s"); kv_mm(1, 7); kv_out(1, 7, "s"); d_quant(4); kv_mm(1, 4); kv_mm(2, 4)
        kv_out(1, 4, "s"); kv_mm(3, 4); d_inter_v(5); d_quant(5); kv_mm(1, 5); kv_out(1, 5, "s")
        wr_inter(0, "v"); wr_inter(1, "v"); wr_inter(2, "v"); wr_inter(3, "v"); kv_out(3, 4, "v"); wr_quant()
        kv_mm(0, 5); kv_out(0, 5, "v"); kv_out(2, 4, "v"); kv_mm(3, 5); kv_mm(2, 5); kv_out(3, 5, "s")
        kv_mm(0, 4); kv_out(0, 4, "s"); kr_passes(0); kr_passes(1); rope(0); kv_out(2, 5, "s"); kr_passes(2)
        kr_passes(3); rope(1)
